import numpy as np
import ml_dtypes


def mxq(x, axis, fmt="e4m3"):
    dtype, down = {"e4m3": (ml_dtypes.float8_e4m3fn, 7), "e5m2": (ml_dtypes.float8_e5m2, 14)}[fmt]
    v = np.moveaxis(np.asarray(x, np.float32).astype(ml_dtypes.bfloat16).astype(np.float64), axis, -1)
    blocks = v.reshape(v.shape[:-1] + (-1, 32))
    amax = np.abs(blocks).max(-1, keepdims=True)
    byte = np.maximum(np.where(amax > 0, np.frexp(amax)[1] - 1 + 127, 0) - down, 1)
    scale = np.exp2(byte - 127.0)
    codes = (blocks / scale).astype(np.float32).astype(dtype).astype(np.float64)
    return np.moveaxis((codes * scale).reshape(v.shape), -1, axis)


WIDE = False


def mx_kscale(k):
    if not WIDE:
        return np.ones(k)
    levels = np.array([10, -10, 5, -5, 0])
    a = np.random.permutation(np.resize(levels, k // 512 * 4)).reshape(k // 512, 4)
    idx = np.arange(k)
    return np.exp2(a[idx // 512, idx % 128 // 32])


BF16 = ml_dtypes.bfloat16


def bf(x):
    return np.asarray(x, np.float32).astype(BF16)


def f64(x):
    return np.asarray(x).astype(np.float64)


B, T, L, D, K = 8, 1024, 256, 1024, 256
HS = 0.25


def sigmoid(v):
    return 1.0 / (1.0 + np.exp(-v))


def setup_inputs():
    s = mx_kscale(D)
    return {"H": bf(np.random.standard_normal((B, T, D)) * HS * s),
            "Wr": bf(np.random.standard_normal((K, D)) / (HS * np.sqrt(D)) / s),
            "br": bf(np.random.standard_normal(K) * 0.3)}


def reference(H, Wr, br):
    h = f64(H)
    route = sigmoid((mxq(h, 2, "e4m3") @ mxq(f64(Wr), 1, "e4m3").T) + f64(br))
    return mxq(route, 1, "e4m3").transpose(0, 2, 1) @ mxq(h, 1, "e4m3")

@@ -1,0 +1,260 @@
+from contextlib import ExitStack
+
+import concourse.mybir as mybir
+from concourse.masks import make_identity
+
+F32 = mybir.dt.float32
+BF16 = mybir.dt.bfloat16
+U32 = mybir.dt.uint32
+U8 = mybir.dt.uint8
+FP8X4 = mybir.dt.float8_e4m3fn_x4
+ACT = mybir.ActivationFunctionType
+
+B, T, D, K = 8, 1024, 1024, 256
+P = 128
+UNITS = 2 * B
+HALVES = 2 * B
+FLOPS = 2 * 2 * B * T * D * K
+H_BUFS = 8
+PINNED = True
+
+
+def tile_instrumentspecificslotmemory_pa_t_kernel(tc, H, Wr, br, out):
+    nc = tc.nc
+    with ExitStack() as ctx:
+        const = ctx.enter_context(tc.tile_pool(name="const", bufs=1))
+        hpool = ctx.enter_context(tc.tile_pool(name="hpool", bufs=H_BUFS))
+        work = ctx.enter_context(tc.tile_pool(name="work", bufs=2))
+        psum = ctx.enter_context(tc.psum_pool(name="psum", bufs=8))
+        if PINNED:
+            ctx.enter_context(tc.manual_schedule())
+
+        h_sb = {}
+        g1 = {}
+        c1 = {}
+        s1 = {}
+        r_ps = {}
+        rt = {}
+        y_ps = {}
+        gr = {}
+        rc = {}
+        rs = {}
+        g2 = {}
+        c2 = {}
+        s2 = {}
+        x_ps = {}
+        o_ps = {}
+        o_sb = {}
+
+        def load(u):
+            b, c = divmod(u, 2)
+            h = hpool.tile([P, 4 * D], BF16, name="h", tag="h")
+            h_sb[u] = h
+            rows = H[b, 512 * c : 512 * c + 512, :].rearrange("(p j) d -> p j d", j=4)
+            hv = h[:].rearrange("p (j d) -> p j d", j=4)
+            if u == 0:
+                nc.sync.dma_start(out=hv[:, 0:2, :], in_=rows[:, 0:2, :])
+                nc.sync.dma_start(out=hv[:, 2:4, :], in_=rows[:, 2:4, :])
+            else:
+                nc.sync.dma_start(out=hv, in_=rows)
+
+        w_sb = const.tile([P, 2 * D], BF16, name="w_sb")
+        nc.scalar.dma_start(
+            out=w_sb[:].rearrange("p (kt d) -> p kt d", kt=2),
+            in_=Wr.rearrange("(kt p) d -> p kt d", p=P),
+        )
+        bz = const.tile([P, P], BF16, name="bz")
+        nc.vector.memset(bz[:], 0.0)
+        nc.scalar.dma_start(out=bz[0:2, :], in_=br.rearrange("(kt k) -> kt k", kt=2))
+        warm_in = const.tile([P, 1], F32, name="warm_in")
+        warm_out = const.tile([P, 1], F32, name="warm_out")
+        nc.vector.memset(warm_in[:], 0.0)
+        nc.scalar.activation(out=warm_out[:], in_=warm_in[:], func=ACT.Sigmoid)
+        for u in range(H_BUFS):
+            load(u)
+        ident_f = const.tile([P, P], F32, name="ident_f")
+        make_identity(nc, ident_f[:])
+        ident_b = const.tile([P, P], BF16, name="ident_b")
+        make_identity(nc, ident_b[:])
+        bias = const.tile([P, 2], F32, name="bias")
+        gw = const.tile([P, 2048], BF16, name="gw", align_bytes=64)
+        wc = const.tile([P, 512], U32, name="wc", align_bytes=64)
+        ws = const.tile([P, 512], U8, name="ws", align_bytes=64)
+
+        def prep_weights():
+            ww = w_sb[:].bitcast(F32)
+            gww = gw[:].bitcast(F32).rearrange("p (g kk u) -> p g kk u", g=2, u=2)
+            for g in range(2):
+                xw = psum.tile([P, 2, 2, P], F32, name="xw", tag="bank")
+                for u in range(2):
+                    for kt in range(2):
+                        lo = 512 * kt + 256 * g + 128 * u
+                        nc.tensor.transpose(xw[:, u, kt, :], ww[:, lo : lo + 128], ident_f[:])
+                nc.vector.tensor_copy(
+                    out=gww[:, g, :, :].rearrange("p (kt k) u -> p kt k u", kt=2),
+                    in_=xw[:].rearrange("p u kt k -> p kt k u"),
+                )
+            yb = psum.tile([P, 4, 256], BF16, name="yb", tag="bank")
+            nc.tensor.transpose(yb[:, 0, 0:P], bz[:], ident_b[:])
+            nc.vector.tensor_copy(out=bias[:], in_=yb[:, 0, 0:2])
+            nc.vector.quantize_mx(out=wc[:].bitcast(FP8X4), scales=ws[:], in_=gw[:])
+
+        def transpose_h(u):
+            hw = h_sb[u][:].bitcast(F32)
+            for g in range(2):
+                for jp in range(2):
+                    x = psum.tile([P, 2, 2, P], F32, name="x", tag="bank")
+                    x_ps[(u, g, jp)] = x
+                    for jl in range(2):
+                        for w in range(2):
+                            lo = 512 * (2 * jp + jl) + 256 * g + 128 * w
+                            nc.tensor.transpose(x[:, jl, w, :], hw[:, lo : lo + 128], ident_f[:])
+
+        def copy_x(u, g, jp, eng):
+            if (g, jp) == (0, 0):
+                g1[u] = work.tile([P, 4096], BF16, name="g1", tag="g1", align_bytes=64)
+            gv = g1[u][:].bitcast(F32).rearrange("p (g c w) -> p g c w", g=2, w=2)
+            dst = gv[:, g, 256 * jp : 256 * jp + 256, :].rearrange("p (jl q) w -> p jl q w", jl=2)
+            src = x_ps[(u, g, jp)][:].rearrange("p jl w q -> p jl q w")
+            if eng == "s":
+                nc.scalar.copy(out=dst, in_=src)
+            else:
+                nc.vector.tensor_copy(out=dst, in_=src)
+
+        def quant_g1(u):
+            c1[u] = work.tile([P, 1024], U32, name="c1", tag="c1", align_bytes=64)
+            s1[u] = work.tile([P, 1024], U8, name="s1", tag="s1", align_bytes=64)
+            nc.vector.quantize_mx(out=c1[u][:].bitcast(FP8X4), scales=s1[u][:], in_=g1[u][:])
+
+        def mm1(u):
+            for kt in range(2):
+                r = psum.tile([P, 512], F32, name="r", tag="bank")
+                r_ps[(u, kt)] = r
+                for g in range(2):
+                    lo = 256 * g + 128 * kt
+                    nc.tensor.matmul_mx(
+                        out=r[:],
+                        lhsT=wc[:, lo : lo + 128].bitcast(FP8X4),
+                        lhsT_scale=ws[:, lo : lo + 128],
+                        rhs=c1[u][:, 512 * g : 512 * g + 512].bitcast(FP8X4),
+                        rhs_scale=s1[u][:, 512 * g : 512 * g + 512],
+                        start=(g == 0),
+                        stop=(g == 1),
+                    )
+
+        def sigmoid(u):
+            rt[u] = work.tile([P, 1024], BF16, name="rt", tag="rt", bufs=3)
+            for kt in range(2):
+                nc.scalar.activation(
+                    out=rt[u][:, 512 * kt : 512 * kt + 512],
+                    in_=r_ps[(u, kt)][:],
+                    func=ACT.Sigmoid,
+                    bias=bias[:, kt : kt + 1],
+                    scale=1.0,
+                )
+
+        def transpose_r(u):
+            y = psum.tile([P, 4, 256], BF16, name="y", tag="bank")
+            y_ps[u] = y
+            for kt in range(2):
+                for j in range(4):
+                    lo = 512 * kt + 128 * j
+                    nc.tensor.transpose(y[:, j, 128 * kt : 128 * kt + 128], rt[u][:, lo : lo + 128], ident_b[:])
+
+        def copy_y(u):
+            gr[u] = work.tile([P, 1024], BF16, name="gr", tag="gr", align_bytes=64)
+            nc.scalar.copy(
+                out=gr[u][:].rearrange("p (kk j) -> p kk j", j=4),
+                in_=y_ps[u][:].rearrange("p j kk -> p kk j"),
+            )
+
+        def quant_gr(u):
+            rc[u] = work.tile([P, 256], U32, name="rc", tag="rc", bufs=6, align_bytes=64)
+            rs[u] = work.tile([P, 256], U8, name="rs", tag="rs", bufs=6, align_bytes=64)
+            nc.vector.quantize_mx(out=rc[u][:].bitcast(FP8X4), scales=rs[u][:], in_=gr[u][:])
+
+        def regroup(u, half):
+            if half == 0:
+                g2[u] = work.tile([P, 4096], BF16, name="g2", tag="g2", bufs=3, align_bytes=64)
+            dst = g2[u][:].rearrange("p (c i t) -> p c t i", i=4, t=4)
+            src = h_sb[u][:].rearrange("p (t c i) -> p c t i", t=4, i=4)
+            nc.vector.tensor_copy(
+                out=dst[:, 128 * half : 128 * half + 128], in_=src[:, 128 * half : 128 * half + 128]
+            )
+
+        def quant_g2(u):
+            c2[u] = work.tile([P, 1024], U32, name="c2", tag="c2", bufs=6, align_bytes=64)
+            s2[u] = work.tile([P, 1024], U8, name="s2", tag="s2", bufs=6, align_bytes=64)
+            nc.vector.quantize_mx(out=c2[u][:].bitcast(FP8X4), scales=s2[u][:], in_=g2[u][:])
+
+        def mm2(h):
+            b, kt = divmod(h, 2)
+            for dh in range(2):
+                o = psum.tile([P, 512], F32, name="o", tag="bank")
+                o_ps[(h, dh)] = o
+                for c in range(2):
+                    u = 2 * b + c
+                    nc.tensor.matmul_mx(
+                        out=o[:],
+                        lhsT=rc[u][:, 128 * kt : 128 * kt + 128].bitcast(FP8X4),
+                        lhsT_scale=rs[u][:, 128 * kt : 128 * kt + 128],
+                        rhs=c2[u][:, 512 * dh : 512 * dh + 512].bitcast(FP8X4),
+                        rhs_scale=s2[u][:, 512 * dh : 512 * dh + 512],
+                        start=(c == 0),
+                        stop=(c == 1),
+                    )
+
+        def copy_o(h, dh, eng):
+            if h not in o_sb:
+                o_sb[h] = work.tile([P, 1024], F32, name="o_sb", tag="o_sb", bufs=4)
+            dst = o_sb[h][:, 512 * dh : 512 * dh + 512]
+            src = o_ps[(h, dh)][:]
+            if eng == "s":
+                nc.scalar.copy(out=dst, in_=src)
+            else:
+                nc.vector.tensor_copy(out=dst, in_=src)
+
+        def store(h):
+            b, kt = divmod(h, 2)
+            nc.sync.dma_start(out=out[b, 128 * kt : 128 * kt + 128, :], in_=o_sb[h][:])
+
+        def unit(u):
+            return 0 <= u < UNITS
+
+        for s in range(UNITS + 6):
+            if unit(s - 2):
+                transpose_r(s - 2)
+            if unit(s):
+                transpose_h(s)
+            if s == 0:
+                prep_weights()
+            if unit(s - 1):
+                quant_g1(s - 1)
+            if 0 <= s - 5 < HALVES:
+                copy_o(s - 5, 0, "s")
+                store(s - 5)
+            if unit(s - 2):
+                copy_y(s - 2)
+            if unit(s):
+                copy_x(s, 0, 0, "s")
+                copy_x(s, 0, 1, "s")
+            if unit(s - 1):
+                mm1(s - 1)
+            if 0 <= s - 4 < HALVES:
+                mm2(s - 4)
+            if unit(s - 1):
+                sigmoid(s - 1)
+            if unit(s):
+                copy_x(s, 1, 0, "s")
+                copy_x(s, 1, 1, "s")
+                regroup(s, 0)
+            if unit(s - 2):
+                quant_gr(s - 2)
+            if unit(s):
+                regroup(s, 1)
+            if unit(s - 1):
+                quant_g2(s - 1)
+            if 0 <= s - 4 < HALVES:
+                copy_o(s - 4, 1, "v")
+            if unit(s) and s + H_BUFS < UNITS:
+                load(s + H_BUFS)

@@ -17,6 +17,7 @@ HALVES = 2 * B
 FLOPS = 2 * 2 * B * T * D * K
 H_BUFS = 8
 PINNED = True
+FINE_STORES_FROM = 12
 
 
 def tile_instrumentspecificslotmemory_pa_t_kernel(tc, H, Wr, br, out):
@@ -46,6 +47,8 @@ def tile_instrumentspecificslotmemory_pa_t_kernel(tc, H, Wr, br, out):
         o_ps = {}
         o_sb = {}
 
+        w_sb = const.tile([P, 2 * D], BF16, name="w_sb")
+
         def load(u):
             b, c = divmod(u, 2)
             h = hpool.tile([P, 4 * D], BF16, name="h", tag="h")
@@ -55,14 +58,20 @@ def tile_instrumentspecificslotmemory_pa_t_kernel(tc, H, Wr, br, out):
             if u == 0:
                 nc.sync.dma_start(out=hv[:, 0:2, :], in_=rows[:, 0:2, :])
                 nc.sync.dma_start(out=hv[:, 2:4, :], in_=rows[:, 2:4, :])
+                nc.sync.dma_start(
+                    out=w_sb[:].rearrange("p (kt d) -> p kt d", kt=2),
+                    in_=Wr.rearrange("(kt p) d -> p kt d", p=P),
+                )
             else:
                 nc.sync.dma_start(out=hv, in_=rows)
 
-        w_sb = const.tile([P, 2 * D], BF16, name="w_sb")
-        nc.scalar.dma_start(
-            out=w_sb[:].rearrange("p (kt d) -> p kt d", kt=2),
-            in_=Wr.rearrange("(kt p) d -> p kt d", p=P),
-        )
+        st = {"loaded": 0, "bulk": 0, "t_done": -1, "rg_done": -1, "q2_done": -1, "half": 0}
+
+        def load_to(n):
+            while st["loaded"] < min(n, UNITS):
+                load(st["loaded"])
+                st["loaded"] = st["loaded"] + 1
+
         bz = const.tile([P, P], BF16, name="bz")
         nc.vector.memset(bz[:], 0.0)
         nc.scalar.dma_start(out=bz[0:2, :], in_=br.rearrange("(kt k) -> kt k", kt=2))
@@ -70,8 +79,7 @@ def tile_instrumentspecificslotmemory_pa_t_kernel(tc, H, Wr, br, out):
         warm_out = const.tile([P, 1], F32, name="warm_out")
         nc.vector.memset(warm_in[:], 0.0)
         nc.scalar.activation(out=warm_out[:], in_=warm_in[:], func=ACT.Sigmoid)
-        for u in range(H_BUFS):
-            load(u)
+        load_to(H_BUFS)
         ident_f = const.tile([P, P], F32, name="ident_f")
         make_identity(nc, ident_f[:])
         ident_b = const.tile([P, P], BF16, name="ident_b")
@@ -101,8 +109,8 @@ def tile_instrumentspecificslotmemory_pa_t_kernel(tc, H, Wr, br, out):
 
         def transpose_h(u):
             hw = h_sb[u][:].bitcast(F32)
-            for g in range(2):
-                for jp in range(2):
+            for jp in range(2):
+                for g in range(2):
                     x = psum.tile([P, 2, 2, P], F32, name="x", tag="bank")
                     x_ps[(u, g, jp)] = x
                     for jl in range(2):
@@ -110,8 +118,9 @@ def tile_instrumentspecificslotmemory_pa_t_kernel(tc, H, Wr, br, out):
                             lo = 512 * (2 * jp + jl) + 256 * g + 128 * w
                             nc.tensor.transpose(x[:, jl, w, :], hw[:, lo : lo + 128], ident_f[:])
 
-        def copy_x(u, g, jp, eng):
-            if (g, jp) == (0, 0):
+        def copy_x(u, i, eng):
+            jp, g = divmod(i, 2)
+            if i == 0:
                 g1[u] = work.tile([P, 4096], BF16, name="g1", tag="g1", align_bytes=64)
             gv = g1[u][:].bitcast(F32).rearrange("p (g c w) -> p g c w", g=2, w=2)
             dst = gv[:, g, 256 * jp : 256 * jp + 256, :].rearrange("p (jl q) w -> p jl q w", jl=2)
@@ -173,14 +182,16 @@ def tile_instrumentspecificslotmemory_pa_t_kernel(tc, H, Wr, br, out):
             rs[u] = work.tile([P, 256], U8, name="rs", tag="rs", bufs=6, align_bytes=64)
             nc.vector.quantize_mx(out=rc[u][:].bitcast(FP8X4), scales=rs[u][:], in_=gr[u][:])
 
-        def regroup(u, half):
+        def regroup(u, half, eng):
             if half == 0:
                 g2[u] = work.tile([P, 4096], BF16, name="g2", tag="g2", bufs=3, align_bytes=64)
             dst = g2[u][:].rearrange("p (c i t) -> p c t i", i=4, t=4)
             src = h_sb[u][:].rearrange("p (t c i) -> p c t i", t=4, i=4)
-            nc.vector.tensor_copy(
-                out=dst[:, 128 * half : 128 * half + 128], in_=src[:, 128 * half : 128 * half + 128]
-            )
+            cols = slice(128 * half, 128 * half + 128)
+            if eng == "s":
+                nc.scalar.copy(out=dst[:, cols], in_=src[:, cols])
+            else:
+                nc.vector.tensor_copy(out=dst[:, cols], in_=src[:, cols])
 
         def quant_g2(u):
             c2[u] = work.tile([P, 1024], U32, name="c2", tag="c2", bufs=6, align_bytes=64)
@@ -216,45 +227,83 @@ def tile_instrumentspecificslotmemory_pa_t_kernel(tc, H, Wr, br, out):
 
         def store(h):
             b, kt = divmod(h, 2)
-            nc.sync.dma_start(out=out[b, 128 * kt : 128 * kt + 128, :], in_=o_sb[h][:])
+            rows = out[b, 128 * kt : 128 * kt + 128, :]
+            if h >= FINE_STORES_FROM:
+                for dh in range(2):
+                    nc.sync.dma_start(
+                        out=rows[:, 512 * dh : 512 * dh + 512], in_=o_sb[h][:, 512 * dh : 512 * dh + 512]
+                    )
+            else:
+                nc.sync.dma_start(out=rows, in_=o_sb[h][:])
+
+        bulk = []
+        for u in range(UNITS):
+            bulk.extend([("rg", u, 0), ("rg", u, 1), ("q", u, 0)])
+
+        def do_bulk(n):
+            for i in range(n):
+                if st["bulk"] < len(bulk):
+                    kind, u, half = bulk[st["bulk"]]
+                    st["bulk"] = st["bulk"] + 1
+                    if kind == "rg":
+                        regroup(u, half, "s" if 2 * u + half in (1, 2) else "v")
+                        if half == 1:
+                            st["rg_done"] = u
+                    else:
+                        quant_g2(u)
+                        st["q2_done"] = u
 
         def unit(u):
             return 0 <= u < UNITS
 
-        for s in range(UNITS + 6):
+        pending = []
+        for s in range(UNITS + 14):
             if unit(s - 2):
                 transpose_r(s - 2)
             if unit(s):
                 transpose_h(s)
+                st["t_done"] = s
             if s == 0:
+                do_bulk(1)
                 prep_weights()
             if unit(s - 1):
                 quant_g1(s - 1)
-            if 0 <= s - 5 < HALVES:
-                copy_o(s - 5, 0, "s")
-                store(s - 5)
+            for h, dh in pending:
+                copy_o(h, dh, "s")
+            for h in sorted(set([hd[0] for hd in pending])):
+                store(h)
+            pending = []
             if unit(s - 2):
                 copy_y(s - 2)
             if unit(s):
-                copy_x(s, 0, 0, "s")
-                copy_x(s, 0, 1, "s")
+                copy_x(s, 0, "s")
+                copy_x(s, 1, "s")
             if unit(s - 1):
                 mm1(s - 1)
-            if 0 <= s - 4 < HALVES:
-                mm2(s - 4)
+            here = []
+            limit = 2 if s > UNITS else 1
+            while st["half"] < HALVES and len(here) < limit:
+                last_unit = 2 * (st["half"] // 2) + 1
+                if last_unit + 3 > s or st["q2_done"] < last_unit:
+                    break
+                mm2(st["half"])
+                here.append(st["half"])
+                st["half"] = st["half"] + 1
             if unit(s - 1):
                 sigmoid(s - 1)
+            light = s < UNITS and s % 4 == 1
             if unit(s):
-                copy_x(s, 1, 0, "s")
-                copy_x(s, 1, 1, "s")
-                regroup(s, 0)
+                copy_x(s, 2, "v" if light else "s")
+                copy_x(s, 3, "v" if light else "s")
+            n = 2 if light else 3
+            do_bulk((n + 1) // 2)
             if unit(s - 2):
                 quant_gr(s - 2)
-            if unit(s):
-                regroup(s, 1)
-            if unit(s - 1):
-                quant_g2(s - 1)
-            if 0 <= s - 4 < HALVES:
-                copy_o(s - 4, 1, "v")
-            if unit(s) and s + H_BUFS < UNITS:
-                load(s + H_BUFS)
+            do_bulk(n // 2)
+            for h in here:
+                if h % 2 == 0 or s >= UNITS:
+                    copy_o(h, 1, "v")
+                    pending.append((h, 0))
+                else:
+                    pending.extend([(h, 0), (h, 1)])
+            load_to(min(st["t_done"], st["rg_done"]) + 1 + H_BUFS)

@@ -107,16 +107,15 @@ def tile_instrumentspecificslotmemory_pa_t_kernel(tc, H, Wr, br, out):
             nc.vector.tensor_copy(out=bias[:], in_=yb[:, 0, 0:2])
             nc.vector.quantize_mx(out=wc[:].bitcast(FP8X4), scales=ws[:], in_=gw[:])
 
-        def transpose_h(u):
+        def transpose_h(u, jp):
             hw = h_sb[u][:].bitcast(F32)
-            for jp in range(2):
-                for g in range(2):
-                    x = psum.tile([P, 2, 2, P], F32, name="x", tag="bank")
-                    x_ps[(u, g, jp)] = x
-                    for jl in range(2):
-                        for w in range(2):
-                            lo = 512 * (2 * jp + jl) + 256 * g + 128 * w
-                            nc.tensor.transpose(x[:, jl, w, :], hw[:, lo : lo + 128], ident_f[:])
+            for g in range(2):
+                x = psum.tile([P, 2, 2, P], F32, name="x", tag="bank")
+                x_ps[(u, g, jp)] = x
+                for jl in range(2):
+                    for w in range(2):
+                        lo = 512 * (2 * jp + jl) + 256 * g + 128 * w
+                        nc.tensor.transpose(x[:, jl, w, :], hw[:, lo : lo + 128], ident_f[:])
 
         def copy_x(u, i, eng):
             jp, g = divmod(i, 2)
@@ -258,28 +257,36 @@ def tile_instrumentspecificslotmemory_pa_t_kernel(tc, H, Wr, br, out):
 
         pending = []
         for s in range(UNITS + 14):
-            if unit(s - 2):
-                transpose_r(s - 2)
+            light = s < UNITS and s % 4 == 1
+            n = 2 if light else 3
             if unit(s):
-                transpose_h(s)
-                st["t_done"] = s
-            if s == 0:
-                do_bulk(1)
-                prep_weights()
-            if unit(s - 1):
-                quant_g1(s - 1)
+                transpose_h(s, 0)
             for h, dh in pending:
                 copy_o(h, dh, "s")
             for h in sorted(set([hd[0] for hd in pending])):
                 store(h)
             pending = []
-            if unit(s - 2):
-                copy_y(s - 2)
             if unit(s):
                 copy_x(s, 0, "s")
                 copy_x(s, 1, "s")
+                transpose_h(s, 1)
+                st["t_done"] = s
+            if s == 0:
+                do_bulk(1)
+                prep_weights()
+            if unit(s - 2):
+                transpose_r(s - 2)
+            if unit(s - 1):
+                quant_g1(s - 1)
+            if unit(s - 2):
+                copy_y(s - 2)
+            do_bulk((n + 1) // 2)
+            if unit(s):
+                copy_x(s, 2, "v" if light else "s")
+                copy_x(s, 3, "v" if light else "s")
             if unit(s - 1):
                 mm1(s - 1)
+            do_bulk(n // 2)
             here = []
             limit = 2 if s > UNITS else 1
             while st["half"] < HALVES and len(here) < limit:
@@ -289,21 +296,14 @@ def tile_instrumentspecificslotmemory_pa_t_kernel(tc, H, Wr, br, out):
                 mm2(st["half"])
                 here.append(st["half"])
                 st["half"] = st["half"] + 1
-            if unit(s - 1):
-                sigmoid(s - 1)
-            light = s < UNITS and s % 4 == 1
-            if unit(s):
-                copy_x(s, 2, "v" if light else "s")
-                copy_x(s, 3, "v" if light else "s")
-            n = 2 if light else 3
-            do_bulk((n + 1) // 2)
             if unit(s - 2):
                 quant_gr(s - 2)
-            do_bulk(n // 2)
             for h in here:
                 if h % 2 == 0 or s >= UNITS:
                     copy_o(h, 1, "v")
                     pending.append((h, 0))
                 else:
                     pending.extend([(h, 0), (h, 1)])
+            if unit(s - 1):
+                sigmoid(s - 1)
             load_to(min(st["t_done"], st["rg_done"]) + 1 + H_BUFS)

@@ -269,15 +269,16 @@ def tile_instrumentspecificslotmemory_pa_t_kernel(tc, H, Wr, br, out):
             if unit(s):
                 copy_x(s, 0, "s")
                 copy_x(s, 1, "s")
+            if unit(s - 1):
+                quant_g1(s - 1)
+            if unit(s - 2):
+                transpose_r(s - 2)
+            if unit(s):
                 transpose_h(s, 1)
                 st["t_done"] = s
             if s == 0:
                 do_bulk(1)
                 prep_weights()
-            if unit(s - 2):
-                transpose_r(s - 2)
-            if unit(s - 1):
-                quant_g1(s - 1)
             if unit(s - 2):
                 copy_y(s - 2)
             do_bulk((n + 1) // 2)
@@ -286,7 +287,6 @@ def tile_instrumentspecificslotmemory_pa_t_kernel(tc, H, Wr, br, out):
                 copy_x(s, 3, "v" if light else "s")
             if unit(s - 1):
                 mm1(s - 1)
-            do_bulk(n // 2)
             here = []
             limit = 2 if s > UNITS else 1
             while st["half"] < HALVES and len(here) < limit:
@@ -296,10 +296,11 @@ def tile_instrumentspecificslotmemory_pa_t_kernel(tc, H, Wr, br, out):
                 mm2(st["half"])
                 here.append(st["half"])
                 st["half"] = st["half"] + 1
+            do_bulk(n // 2)
             if unit(s - 2):
                 quant_gr(s - 2)
             for h in here:
-                if h % 2 == 0 or s >= UNITS:
+                if h % 4 == 0 or s >= UNITS:
                     copy_o(h, 1, "v")
                     pending.append((h, 0))
                 else:

@@ -235,9 +235,10 @@ def tile_instrumentspecificslotmemory_pa_t_kernel(tc, H, Wr, br, out):
             else:
                 nc.sync.dma_start(out=rows, in_=o_sb[h][:])
 
-        bulk = []
-        for u in range(UNITS):
-            bulk.extend([("rg", u, 0), ("rg", u, 1), ("q", u, 0)])
+        bulk = [("rg", 0, 0), ("rg", 0, 1)]
+        for u in range(1, UNITS):
+            bulk.extend([("rg", u, 0), ("q", u - 1, 0), ("rg", u, 1)])
+        bulk.append(("q", UNITS - 1, 0))
 
         def do_bulk(n):
             for i in range(n):
@@ -257,7 +258,7 @@ def tile_instrumentspecificslotmemory_pa_t_kernel(tc, H, Wr, br, out):
 
         pending = []
         for s in range(UNITS + 14):
-            light = s < UNITS and s % 4 == 1
+            light = s < UNITS and s % 4 == 0
             n = 2 if light else 3
             if unit(s):
                 transpose_h(s, 0)

@@ -301,7 +301,7 @@ def tile_instrumentspecificslotmemory_pa_t_kernel(tc, H, Wr, br, out):
             if unit(s - 2):
                 quant_gr(s - 2)
             for h in here:
-                if h % 4 == 0 or s >= UNITS:
+                if s >= UNITS:
                     copy_o(h, 1, "v")
                     pending.append((h, 0))
                 else:

@@ -13,299 +13,299 @@ ACT = mybir.ActivationFunctionType
 B, T, D, K = 8, 1024, 1024, 256
 P = 128
 UNITS = 2 * B
-HALVES = 2 * B
+SLABS = 2 * B
 FLOPS = 2 * 2 * B * T * D * K
+
 H_BUFS = 8
-PINNED = True
-FINE_STORES_FROM = 12
+CODE_BUFS = 6
+FINE_STORES_FROM = SLABS - 4
+LIGHT_EVERY = 4
 
 
 def tile_instrumentspecificslotmemory_pa_t_kernel(tc, H, Wr, br, out):
     nc = tc.nc
     with ExitStack() as ctx:
         const = ctx.enter_context(tc.tile_pool(name="const", bufs=1))
-        hpool = ctx.enter_context(tc.tile_pool(name="hpool", bufs=H_BUFS))
+        h_pool = ctx.enter_context(tc.tile_pool(name="h_pool", bufs=H_BUFS))
         work = ctx.enter_context(tc.tile_pool(name="work", bufs=2))
         psum = ctx.enter_context(tc.psum_pool(name="psum", bufs=8))
-        if PINNED:
-            ctx.enter_context(tc.manual_schedule())
+        ctx.enter_context(tc.manual_schedule())
 
-        h_sb = {}
-        g1 = {}
-        c1 = {}
-        s1 = {}
-        r_ps = {}
-        rt = {}
-        y_ps = {}
-        gr = {}
-        rc = {}
-        rs = {}
-        g2 = {}
-        c2 = {}
-        s2 = {}
-        x_ps = {}
-        o_ps = {}
-        o_sb = {}
+        h_sb, ht_bank, ht_grouped, ht_codes, ht_scales = {}, {}, {}, {}, {}
+        sum_bank, route_t, route_bank, route_grouped, route_codes, route_scales = {}, {}, {}, {}, {}, {}
+        h_grouped, h_codes, h_scales = {}, {}, {}
+        agg_bank, agg_sb = {}, {}
+
+        progress = {"loaded": 0, "regroup": 0, "transposed": -1, "regrouped": -1, "h_quantised": -1,
+                    "multiplied": 0, "stored": 0}
+
+        def copy_on(engine, dst, src):
+            if engine == "scalar":
+                nc.scalar.copy(out=dst, in_=src)
+            else:
+                nc.vector.tensor_copy(out=dst, in_=src)
 
         w_sb = const.tile([P, 2 * D], BF16, name="w_sb")
 
         def load(u):
             b, c = divmod(u, 2)
-            h = hpool.tile([P, 4 * D], BF16, name="h", tag="h")
-            h_sb[u] = h
+            h_sb[u] = h_pool.tile([P, 4 * D], BF16, name="h_sb", tag="h_sb")
             rows = H[b, 512 * c : 512 * c + 512, :].rearrange("(p j) d -> p j d", j=4)
-            hv = h[:].rearrange("p (j d) -> p j d", j=4)
+            dst = h_sb[u][:].rearrange("p (j d) -> p j d", j=4)
             if u == 0:
-                nc.sync.dma_start(out=hv[:, 0:2, :], in_=rows[:, 0:2, :])
-                nc.sync.dma_start(out=hv[:, 2:4, :], in_=rows[:, 2:4, :])
+                nc.sync.dma_start(out=dst[:, 0:2, :], in_=rows[:, 0:2, :])
+                nc.sync.dma_start(out=dst[:, 2:4, :], in_=rows[:, 2:4, :])
                 nc.sync.dma_start(
                     out=w_sb[:].rearrange("p (kt d) -> p kt d", kt=2),
                     in_=Wr.rearrange("(kt p) d -> p kt d", p=P),
                 )
             else:
-                nc.sync.dma_start(out=hv, in_=rows)
+                nc.sync.dma_start(out=dst, in_=rows)
 
-        st = {"loaded": 0, "bulk": 0, "t_done": -1, "rg_done": -1, "q2_done": -1, "half": 0}
+        def load_up_to(n):
+            while progress["loaded"] < min(n, UNITS):
+                load(progress["loaded"])
+                progress["loaded"] = progress["loaded"] + 1
 
-        def load_to(n):
-            while st["loaded"] < min(n, UNITS):
-                load(st["loaded"])
-                st["loaded"] = st["loaded"] + 1
-
-        bz = const.tile([P, P], BF16, name="bz")
-        nc.vector.memset(bz[:], 0.0)
-        nc.scalar.dma_start(out=bz[0:2, :], in_=br.rearrange("(kt k) -> kt k", kt=2))
+        bias_rows = const.tile([P, P], BF16, name="bias_rows")
+        nc.vector.memset(bias_rows[:], 0.0)
+        nc.scalar.dma_start(out=bias_rows[0:2, :], in_=br.rearrange("(kt k) -> kt k", kt=2))
         warm_in = const.tile([P, 1], F32, name="warm_in")
         warm_out = const.tile([P, 1], F32, name="warm_out")
         nc.vector.memset(warm_in[:], 0.0)
         nc.scalar.activation(out=warm_out[:], in_=warm_in[:], func=ACT.Sigmoid)
-        load_to(H_BUFS)
-        ident_f = const.tile([P, P], F32, name="ident_f")
-        make_identity(nc, ident_f[:])
-        ident_b = const.tile([P, P], BF16, name="ident_b")
-        make_identity(nc, ident_b[:])
+        load_up_to(H_BUFS)
+        ident_f32 = const.tile([P, P], F32, name="ident_f32")
+        make_identity(nc, ident_f32[:])
+        ident_bf16 = const.tile([P, P], BF16, name="ident_bf16")
+        make_identity(nc, ident_bf16[:])
         bias = const.tile([P, 2], F32, name="bias")
-        gw = const.tile([P, 2048], BF16, name="gw", align_bytes=64)
-        wc = const.tile([P, 512], U32, name="wc", align_bytes=64)
-        ws = const.tile([P, 512], U8, name="ws", align_bytes=64)
+        w_grouped = const.tile([P, 2048], BF16, name="w_grouped", align_bytes=64)
+        w_codes = const.tile([P, 512], U32, name="w_codes", align_bytes=64)
+        w_scales = const.tile([P, 512], U8, name="w_scales", align_bytes=64)
 
-        def prep_weights():
-            ww = w_sb[:].bitcast(F32)
-            gww = gw[:].bitcast(F32).rearrange("p (g kk u) -> p g kk u", g=2, u=2)
+        def prepare_weights():
+            words = w_sb[:].bitcast(F32)
+            grouped = w_grouped[:].bitcast(F32).rearrange("p (g k blk) -> p g k blk", g=2, blk=2)
             for g in range(2):
-                xw = psum.tile([P, 2, 2, P], F32, name="xw", tag="bank")
-                for u in range(2):
+                bank = psum.tile([P, 2, 2, P], F32, name="w_bank", tag="bank")
+                for blk in range(2):
                     for kt in range(2):
-                        lo = 512 * kt + 256 * g + 128 * u
-                        nc.tensor.transpose(xw[:, u, kt, :], ww[:, lo : lo + 128], ident_f[:])
+                        lo = 512 * kt + 256 * g + 128 * blk
+                        nc.tensor.transpose(bank[:, blk, kt, :], words[:, lo : lo + 128], ident_f32[:])
                 nc.vector.tensor_copy(
-                    out=gww[:, g, :, :].rearrange("p (kt k) u -> p kt k u", kt=2),
-                    in_=xw[:].rearrange("p u kt k -> p kt k u"),
+                    out=grouped[:, g, :, :].rearrange("p (kt k) blk -> p kt k blk", kt=2),
+                    in_=bank[:].rearrange("p blk kt k -> p kt k blk"),
                 )
-            yb = psum.tile([P, 4, 256], BF16, name="yb", tag="bank")
-            nc.tensor.transpose(yb[:, 0, 0:P], bz[:], ident_b[:])
-            nc.vector.tensor_copy(out=bias[:], in_=yb[:, 0, 0:2])
-            nc.vector.quantize_mx(out=wc[:].bitcast(FP8X4), scales=ws[:], in_=gw[:])
+            bank = psum.tile([P, 4, 256], BF16, name="bias_bank", tag="bank")
+            nc.tensor.transpose(bank[:, 0, 0:P], bias_rows[:], ident_bf16[:])
+            nc.vector.tensor_copy(out=bias[:], in_=bank[:, 0, 0:2])
+            nc.vector.quantize_mx(out=w_codes[:].bitcast(FP8X4), scales=w_scales[:], in_=w_grouped[:])
 
         def transpose_h(u, jp):
-            hw = h_sb[u][:].bitcast(F32)
+            words = h_sb[u][:].bitcast(F32)
             for g in range(2):
-                x = psum.tile([P, 2, 2, P], F32, name="x", tag="bank")
-                x_ps[(u, g, jp)] = x
+                bank = psum.tile([P, 2, 2, P], F32, name="ht_bank", tag="bank")
+                ht_bank[(u, g, jp)] = bank
                 for jl in range(2):
-                    for w in range(2):
-                        lo = 512 * (2 * jp + jl) + 256 * g + 128 * w
-                        nc.tensor.transpose(x[:, jl, w, :], hw[:, lo : lo + 128], ident_f[:])
+                    for blk in range(2):
+                        lo = 512 * (2 * jp + jl) + 256 * g + 128 * blk
+                        nc.tensor.transpose(bank[:, jl, blk, :], words[:, lo : lo + 128], ident_f32[:])
 
-        def copy_x(u, i, eng):
-            jp, g = divmod(i, 2)
-            if i == 0:
-                g1[u] = work.tile([P, 4096], BF16, name="g1", tag="g1", align_bytes=64)
-            gv = g1[u][:].bitcast(F32).rearrange("p (g c w) -> p g c w", g=2, w=2)
-            dst = gv[:, g, 256 * jp : 256 * jp + 256, :].rearrange("p (jl q) w -> p jl q w", jl=2)
-            src = x_ps[(u, g, jp)][:].rearrange("p jl w q -> p jl q w")
-            if eng == "s":
-                nc.scalar.copy(out=dst, in_=src)
-            else:
-                nc.vector.tensor_copy(out=dst, in_=src)
+        def copy_ht(u, jp, g, engine):
+            if (jp, g) == (0, 0):
+                ht_grouped[u] = work.tile([P, 4096], BF16, name="ht_grouped", tag="ht_grouped", align_bytes=64)
+            grouped = ht_grouped[u][:].bitcast(F32).rearrange("p (g col blk) -> p g col blk", g=2, blk=2)
+            copy_on(
+                engine,
+                grouped[:, g, 256 * jp : 256 * jp + 256, :].rearrange("p (jl q) blk -> p jl q blk", jl=2),
+                ht_bank[(u, g, jp)][:].rearrange("p jl blk q -> p jl q blk"),
+            )
 
-        def quant_g1(u):
-            c1[u] = work.tile([P, 1024], U32, name="c1", tag="c1", align_bytes=64)
-            s1[u] = work.tile([P, 1024], U8, name="s1", tag="s1", align_bytes=64)
-            nc.vector.quantize_mx(out=c1[u][:].bitcast(FP8X4), scales=s1[u][:], in_=g1[u][:])
+        def quantise_ht(u):
+            ht_codes[u] = work.tile([P, 1024], U32, name="ht_codes", tag="ht_codes", align_bytes=64)
+            ht_scales[u] = work.tile([P, 1024], U8, name="ht_scales", tag="ht_scales", align_bytes=64)
+            nc.vector.quantize_mx(
+                out=ht_codes[u][:].bitcast(FP8X4), scales=ht_scales[u][:], in_=ht_grouped[u][:]
+            )
 
-        def mm1(u):
+        def first_matmul(u):
             for kt in range(2):
-                r = psum.tile([P, 512], F32, name="r", tag="bank")
-                r_ps[(u, kt)] = r
+                bank = psum.tile([P, 512], F32, name="sum_bank", tag="bank")
+                sum_bank[(u, kt)] = bank
                 for g in range(2):
-                    lo = 256 * g + 128 * kt
+                    slots = slice(256 * g + 128 * kt, 256 * g + 128 * kt + 128)
+                    cols = slice(512 * g, 512 * g + 512)
                     nc.tensor.matmul_mx(
-                        out=r[:],
-                        lhsT=wc[:, lo : lo + 128].bitcast(FP8X4),
-                        lhsT_scale=ws[:, lo : lo + 128],
-                        rhs=c1[u][:, 512 * g : 512 * g + 512].bitcast(FP8X4),
-                        rhs_scale=s1[u][:, 512 * g : 512 * g + 512],
+                        out=bank[:],
+                        lhsT=w_codes[:, slots].bitcast(FP8X4),
+                        lhsT_scale=w_scales[:, slots],
+                        rhs=ht_codes[u][:, cols].bitcast(FP8X4),
+                        rhs_scale=ht_scales[u][:, cols],
                         start=(g == 0),
                         stop=(g == 1),
                     )
 
         def sigmoid(u):
-            rt[u] = work.tile([P, 1024], BF16, name="rt", tag="rt", bufs=3)
+            route_t[u] = work.tile([P, 1024], BF16, name="route_t", tag="route_t", bufs=3)
             for kt in range(2):
                 nc.scalar.activation(
-                    out=rt[u][:, 512 * kt : 512 * kt + 512],
-                    in_=r_ps[(u, kt)][:],
+                    out=route_t[u][:, 512 * kt : 512 * kt + 512],
+                    in_=sum_bank[(u, kt)][:],
                     func=ACT.Sigmoid,
                     bias=bias[:, kt : kt + 1],
                     scale=1.0,
                 )
 
-        def transpose_r(u):
-            y = psum.tile([P, 4, 256], BF16, name="y", tag="bank")
-            y_ps[u] = y
+        def transpose_route(u):
+            bank = psum.tile([P, 4, 256], BF16, name="route_bank", tag="bank")
+            route_bank[u] = bank
             for kt in range(2):
                 for j in range(4):
                     lo = 512 * kt + 128 * j
-                    nc.tensor.transpose(y[:, j, 128 * kt : 128 * kt + 128], rt[u][:, lo : lo + 128], ident_b[:])
+                    nc.tensor.transpose(
+                        bank[:, j, 128 * kt : 128 * kt + 128], route_t[u][:, lo : lo + 128], ident_bf16[:]
+                    )
 
-        def copy_y(u):
-            gr[u] = work.tile([P, 1024], BF16, name="gr", tag="gr", align_bytes=64)
+        def copy_route(u):
+            route_grouped[u] = work.tile([P, 1024], BF16, name="route_grouped", tag="route_grouped", align_bytes=64)
             nc.scalar.copy(
-                out=gr[u][:].rearrange("p (kk j) -> p kk j", j=4),
-                in_=y_ps[u][:].rearrange("p j kk -> p kk j"),
+                out=route_grouped[u][:].rearrange("p (k j) -> p k j", j=4),
+                in_=route_bank[u][:].rearrange("p j k -> p k j"),
             )
 
-        def quant_gr(u):
-            rc[u] = work.tile([P, 256], U32, name="rc", tag="rc", bufs=6, align_bytes=64)
-            rs[u] = work.tile([P, 256], U8, name="rs", tag="rs", bufs=6, align_bytes=64)
-            nc.vector.quantize_mx(out=rc[u][:].bitcast(FP8X4), scales=rs[u][:], in_=gr[u][:])
+        def quantise_route(u):
+            route_codes[u] = work.tile(
+                [P, 256], U32, name="route_codes", tag="route_codes", bufs=CODE_BUFS, align_bytes=64
+            )
+            route_scales[u] = work.tile(
+                [P, 256], U8, name="route_scales", tag="route_scales", bufs=CODE_BUFS, align_bytes=64
+            )
+            nc.vector.quantize_mx(
+                out=route_codes[u][:].bitcast(FP8X4), scales=route_scales[u][:], in_=route_grouped[u][:]
+            )
 
-        def regroup(u, half, eng):
-            if half == 0:
-                g2[u] = work.tile([P, 4096], BF16, name="g2", tag="g2", bufs=3, align_bytes=64)
-            dst = g2[u][:].rearrange("p (c i t) -> p c t i", i=4, t=4)
-            src = h_sb[u][:].rearrange("p (t c i) -> p c t i", t=4, i=4)
-            cols = slice(128 * half, 128 * half + 128)
-            if eng == "s":
-                nc.scalar.copy(out=dst[:, cols], in_=src[:, cols])
-            else:
-                nc.vector.tensor_copy(out=dst[:, cols], in_=src[:, cols])
+        def regroup_h(u, g, engine):
+            if g == 0:
+                h_grouped[u] = work.tile([P, 4096], BF16, name="h_grouped", tag="h_grouped", bufs=3, align_bytes=64)
+            dst = h_grouped[u][:].rearrange("p (run i j) -> p run j i", i=4, j=4)
+            src = h_sb[u][:].rearrange("p (j run i) -> p run j i", j=4, i=4)
+            runs = slice(128 * g, 128 * g + 128)
+            copy_on(engine, dst[:, runs], src[:, runs])
 
-        def quant_g2(u):
-            c2[u] = work.tile([P, 1024], U32, name="c2", tag="c2", bufs=6, align_bytes=64)
-            s2[u] = work.tile([P, 1024], U8, name="s2", tag="s2", bufs=6, align_bytes=64)
-            nc.vector.quantize_mx(out=c2[u][:].bitcast(FP8X4), scales=s2[u][:], in_=g2[u][:])
+        def quantise_h(u):
+            h_codes[u] = work.tile([P, 1024], U32, name="h_codes", tag="h_codes", bufs=CODE_BUFS, align_bytes=64)
+            h_scales[u] = work.tile([P, 1024], U8, name="h_scales", tag="h_scales", bufs=CODE_BUFS, align_bytes=64)
+            nc.vector.quantize_mx(out=h_codes[u][:].bitcast(FP8X4), scales=h_scales[u][:], in_=h_grouped[u][:])
 
-        def mm2(h):
-            b, kt = divmod(h, 2)
-            for dh in range(2):
-                o = psum.tile([P, 512], F32, name="o", tag="bank")
-                o_ps[(h, dh)] = o
+        def second_matmul(slab):
+            b, kt = divmod(slab, 2)
+            slots = slice(128 * kt, 128 * kt + 128)
+            for g in range(2):
+                bank = psum.tile([P, 512], F32, name="agg_bank", tag="bank")
+                agg_bank[(slab, g)] = bank
+                cols = slice(512 * g, 512 * g + 512)
                 for c in range(2):
                     u = 2 * b + c
                     nc.tensor.matmul_mx(
-                        out=o[:],
-                        lhsT=rc[u][:, 128 * kt : 128 * kt + 128].bitcast(FP8X4),
-                        lhsT_scale=rs[u][:, 128 * kt : 128 * kt + 128],
-                        rhs=c2[u][:, 512 * dh : 512 * dh + 512].bitcast(FP8X4),
-                        rhs_scale=s2[u][:, 512 * dh : 512 * dh + 512],
+                        out=bank[:],
+                        lhsT=route_codes[u][:, slots].bitcast(FP8X4),
+                        lhsT_scale=route_scales[u][:, slots],
+                        rhs=h_codes[u][:, cols].bitcast(FP8X4),
+                        rhs_scale=h_scales[u][:, cols],
                         start=(c == 0),
                         stop=(c == 1),
                     )
 
-        def copy_o(h, dh, eng):
-            if h not in o_sb:
-                o_sb[h] = work.tile([P, 1024], F32, name="o_sb", tag="o_sb", bufs=4)
-            dst = o_sb[h][:, 512 * dh : 512 * dh + 512]
-            src = o_ps[(h, dh)][:]
-            if eng == "s":
-                nc.scalar.copy(out=dst, in_=src)
-            else:
-                nc.vector.tensor_copy(out=dst, in_=src)
+        def copy_agg(slab, g, engine):
+            if slab not in agg_sb:
+                agg_sb[slab] = work.tile([P, 1024], F32, name="agg_sb", tag="agg_sb", bufs=4)
+            copy_on(engine, agg_sb[slab][:, 512 * g : 512 * g + 512], agg_bank[(slab, g)][:])
 
-        def store(h):
-            b, kt = divmod(h, 2)
+        def store(slab):
+            b, kt = divmod(slab, 2)
             rows = out[b, 128 * kt : 128 * kt + 128, :]
-            if h >= FINE_STORES_FROM:
-                for dh in range(2):
-                    nc.sync.dma_start(
-                        out=rows[:, 512 * dh : 512 * dh + 512], in_=o_sb[h][:, 512 * dh : 512 * dh + 512]
-                    )
+            if slab >= FINE_STORES_FROM:
+                for g in range(2):
+                    cols = slice(512 * g, 512 * g + 512)
+                    nc.sync.dma_start(out=rows[:, cols], in_=agg_sb[slab][:, cols])
             else:
-                nc.sync.dma_start(out=rows, in_=o_sb[h][:])
+                nc.sync.dma_start(out=rows, in_=agg_sb[slab][:])
+            progress["stored"] = progress["stored"] + 1
 
-        bulk = [("rg", 0, 0), ("rg", 0, 1)]
+        regroup_list = [("copy", 0, 0), ("copy", 0, 1)]
         for u in range(1, UNITS):
-            bulk.extend([("rg", u, 0), ("q", u - 1, 0), ("rg", u, 1)])
-        bulk.append(("q", UNITS - 1, 0))
+            regroup_list.extend([("copy", u, 0), ("quantise", u - 1, 0), ("copy", u, 1)])
+        regroup_list.append(("quantise", UNITS - 1, 0))
+        scalar_regroups = ((0, 1), (1, 0))
 
-        def do_bulk(n):
+        def regroup_items(n):
             for i in range(n):
-                if st["bulk"] < len(bulk):
-                    kind, u, half = bulk[st["bulk"]]
-                    st["bulk"] = st["bulk"] + 1
-                    if kind == "rg":
-                        regroup(u, half, "s" if 2 * u + half in (1, 2) else "v")
-                        if half == 1:
-                            st["rg_done"] = u
+                if progress["regroup"] < len(regroup_list):
+                    kind, u, g = regroup_list[progress["regroup"]]
+                    progress["regroup"] = progress["regroup"] + 1
+                    if kind == "copy":
+                        regroup_h(u, g, "scalar" if (u, g) in scalar_regroups else "vector")
+                        if g == 1:
+                            progress["regrouped"] = u
                     else:
-                        quant_g2(u)
-                        st["q2_done"] = u
+                        quantise_h(u)
+                        progress["h_quantised"] = u
 
-        def unit(u):
+        def is_unit(u):
             return 0 <= u < UNITS
 
-        pending = []
-        for s in range(UNITS + 14):
-            light = s < UNITS and s % 4 == 0
-            n = 2 if light else 3
-            if unit(s):
+        waiting = []
+        s = 0
+        while progress["stored"] < SLABS:
+            light = s < UNITS and s % LIGHT_EVERY == 0
+            items = 2 if light else 3
+            if is_unit(s):
                 transpose_h(s, 0)
-            for h, dh in pending:
-                copy_o(h, dh, "s")
-            for h in sorted(set([hd[0] for hd in pending])):
-                store(h)
-            pending = []
-            if unit(s):
-                copy_x(s, 0, "s")
-                copy_x(s, 1, "s")
-            if unit(s - 1):
-                quant_g1(s - 1)
-            if unit(s - 2):
-                transpose_r(s - 2)
-            if unit(s):
+            for slab, g in waiting:
+                copy_agg(slab, g, "scalar")
+            for slab in sorted(set([bank[0] for bank in waiting])):
+                store(slab)
+            waiting = []
+            if is_unit(s):
+                copy_ht(s, 0, 0, "scalar")
+                copy_ht(s, 0, 1, "scalar")
+            if is_unit(s - 1):
+                quantise_ht(s - 1)
+            if is_unit(s - 2):
+                transpose_route(s - 2)
+            if is_unit(s):
                 transpose_h(s, 1)
-                st["t_done"] = s
+                progress["transposed"] = s
             if s == 0:
-                do_bulk(1)
-                prep_weights()
-            if unit(s - 2):
-                copy_y(s - 2)
-            do_bulk((n + 1) // 2)
-            if unit(s):
-                copy_x(s, 2, "v" if light else "s")
-                copy_x(s, 3, "v" if light else "s")
-            if unit(s - 1):
-                mm1(s - 1)
-            here = []
-            limit = 2 if s > UNITS else 1
-            while st["half"] < HALVES and len(here) < limit:
-                last_unit = 2 * (st["half"] // 2) + 1
-                if last_unit + 3 > s or st["q2_done"] < last_unit:
+                regroup_items(1)
+                prepare_weights()
+            if is_unit(s - 2):
+                copy_route(s - 2)
+            regroup_items((items + 1) // 2)
+            if is_unit(s):
+                copy_ht(s, 1, 0, "vector" if light else "scalar")
+                copy_ht(s, 1, 1, "vector" if light else "scalar")
+            if is_unit(s - 1):
+                first_matmul(s - 1)
+            multiplied_here = []
+            while progress["multiplied"] < SLABS and len(multiplied_here) < (2 if s > UNITS else 1):
+                second_unit = 2 * (progress["multiplied"] // 2) + 1
+                if second_unit + 3 > s or progress["h_quantised"] < second_unit:
                     break
-                mm2(st["half"])
-                here.append(st["half"])
-                st["half"] = st["half"] + 1
-            do_bulk(n // 2)
-            if unit(s - 2):
-                quant_gr(s - 2)
-            for h in here:
+                second_matmul(progress["multiplied"])
+                multiplied_here.append(progress["multiplied"])
+                progress["multiplied"] = progress["multiplied"] + 1
+            regroup_items(items // 2)
+            if is_unit(s - 2):
+                quantise_route(s - 2)
+            for slab in multiplied_here:
                 if s >= UNITS:
-                    copy_o(h, 1, "v")
-                    pending.append((h, 0))
+                    copy_agg(slab, 1, "vector")
+                    waiting.append((slab, 0))
                 else:
-                    pending.extend([(h, 0), (h, 1)])
-            if unit(s - 1):
+                    waiting.extend([(slab, 0), (slab, 1)])
+            if is_unit(s - 1):
                 sigmoid(s - 1)
-            load_to(min(st["t_done"], st["rg_done"]) + 1 + H_BUFS)
+            load_up_to(min(progress["transposed"], progress["regrouped"]) + 1 + H_BUFS)
+            s = s + 1

@@ -18,8 +18,7 @@ FLOPS = 2 * 2 * B * T * D * K
 
 H_BUFS = 8
 CODE_BUFS = 6
-FINE_STORES_FROM = SLABS - 4
-LIGHT_EVERY = 4
+ITEMS = 3
 
 
 def tile_instrumentspecificslotmemory_pa_t_kernel(tc, H, Wr, br, out):
@@ -53,12 +52,18 @@ def tile_instrumentspecificslotmemory_pa_t_kernel(tc, H, Wr, br, out):
             rows = H[b, 512 * c : 512 * c + 512, :].rearrange("(p j) d -> p j d", j=4)
             dst = h_sb[u][:].rearrange("p (j d) -> p j d", j=4)
             if u == 0:
-                nc.sync.dma_start(out=dst[:, 0:2, :], in_=rows[:, 0:2, :])
-                nc.sync.dma_start(out=dst[:, 2:4, :], in_=rows[:, 2:4, :])
+                for g in range(2):
+                    for jp in range(2):
+                        piece = (slice(None), slice(2 * jp, 2 * jp + 2), slice(512 * g, 512 * g + 512))
+                        nc.sync.dma_start(out=dst[piece], in_=rows[piece])
                 nc.sync.dma_start(
                     out=w_sb[:].rearrange("p (kt d) -> p kt d", kt=2),
                     in_=Wr.rearrange("(kt p) d -> p kt d", p=P),
                 )
+            elif u == 1:
+                for g in range(2):
+                    piece = (slice(None), slice(None), slice(512 * g, 512 * g + 512))
+                    nc.sync.dma_start(out=dst[piece], in_=rows[piece])
             else:
                 nc.sync.dma_start(out=dst, in_=rows)
 
@@ -102,18 +107,17 @@ def tile_instrumentspecificslotmemory_pa_t_kernel(tc, H, Wr, br, out):
             nc.vector.tensor_copy(out=bias[:], in_=bank[:, 0, 0:2])
             nc.vector.quantize_mx(out=w_codes[:].bitcast(FP8X4), scales=w_scales[:], in_=w_grouped[:])
 
-        def transpose_h(u, jp):
+        def transpose_h(u, jp, g):
             words = h_sb[u][:].bitcast(F32)
-            for g in range(2):
-                bank = psum.tile([P, 2, 2, P], F32, name="ht_bank", tag="bank")
-                ht_bank[(u, g, jp)] = bank
-                for jl in range(2):
-                    for blk in range(2):
-                        lo = 512 * (2 * jp + jl) + 256 * g + 128 * blk
-                        nc.tensor.transpose(bank[:, jl, blk, :], words[:, lo : lo + 128], ident_f32[:])
+            bank = psum.tile([P, 2, 2, P], F32, name="ht_bank", tag="bank")
+            ht_bank[(u, g, jp)] = bank
+            for jl in range(2):
+                for blk in range(2):
+                    lo = 512 * (2 * jp + jl) + 256 * g + 128 * blk
+                    nc.tensor.transpose(bank[:, jl, blk, :], words[:, lo : lo + 128], ident_f32[:])
 
         def copy_ht(u, jp, g, engine):
-            if (jp, g) == (0, 0):
+            if u not in ht_grouped:
                 ht_grouped[u] = work.tile([P, 4096], BF16, name="ht_grouped", tag="ht_grouped", align_bytes=64)
             grouped = ht_grouped[u][:].bitcast(F32).rearrange("p (g col blk) -> p g col blk", g=2, blk=2)
             copy_on(
@@ -150,28 +154,29 @@ def tile_instrumentspecificslotmemory_pa_t_kernel(tc, H, Wr, br, out):
             route_t[u] = work.tile([P, 1024], BF16, name="route_t", tag="route_t", bufs=3)
             for kt in range(2):
                 nc.scalar.activation(
-                    out=route_t[u][:, 512 * kt : 512 * kt + 512],
-                    in_=sum_bank[(u, kt)][:],
+                    out=route_t[u][:, 512 * kt : 512 * kt + 512].rearrange("p (jp q e) -> p jp q e", jp=2, e=2),
+                    in_=sum_bank[(u, kt)][:].rearrange("p (jp e q) -> p jp q e", jp=2, e=2),
                     func=ACT.Sigmoid,
                     bias=bias[:, kt : kt + 1],
                     scale=1.0,
                 )
 
         def transpose_route(u):
-            bank = psum.tile([P, 4, 256], BF16, name="route_bank", tag="bank")
+            words = route_t[u][:].bitcast(F32)
+            bank = psum.tile([P, 2, 256], F32, name="route_bank", tag="bank")
             route_bank[u] = bank
             for kt in range(2):
-                for j in range(4):
-                    lo = 512 * kt + 128 * j
+                for jp in range(2):
+                    lo = 256 * kt + 128 * jp
                     nc.tensor.transpose(
-                        bank[:, j, 128 * kt : 128 * kt + 128], route_t[u][:, lo : lo + 128], ident_bf16[:]
+                        bank[:, jp, 128 * kt : 128 * kt + 128], words[:, lo : lo + 128], ident_f32[:]
                     )
 
         def copy_route(u):
             route_grouped[u] = work.tile([P, 1024], BF16, name="route_grouped", tag="route_grouped", align_bytes=64)
             nc.scalar.copy(
-                out=route_grouped[u][:].rearrange("p (k j) -> p k j", j=4),
-                in_=route_bank[u][:].rearrange("p j k -> p k j"),
+                out=route_grouped[u][:].bitcast(F32).rearrange("p (k jp) -> p k jp", jp=2),
+                in_=route_bank[u][:].rearrange("p jp k -> p k jp"),
             )
 
         def quantise_route(u):
@@ -193,50 +198,47 @@ def tile_instrumentspecificslotmemory_pa_t_kernel(tc, H, Wr, br, out):
             runs = slice(128 * g, 128 * g + 128)
             copy_on(engine, dst[:, runs], src[:, runs])
 
-        def quantise_h(u):
-            h_codes[u] = work.tile([P, 1024], U32, name="h_codes", tag="h_codes", bufs=CODE_BUFS, align_bytes=64)
-            h_scales[u] = work.tile([P, 1024], U8, name="h_scales", tag="h_scales", bufs=CODE_BUFS, align_bytes=64)
-            nc.vector.quantize_mx(out=h_codes[u][:].bitcast(FP8X4), scales=h_scales[u][:], in_=h_grouped[u][:])
+        def quantise_h(u, halves=(0, 1)):
+            if u not in h_codes:
+                h_codes[u] = work.tile([P, 1024], U32, name="h_codes", tag="h_codes", bufs=CODE_BUFS, align_bytes=64)
+                h_scales[u] = work.tile([P, 1024], U8, name="h_scales", tag="h_scales", bufs=CODE_BUFS, align_bytes=64)
+            cols = slice(512 * halves[0], 512 * halves[-1] + 512)
+            nc.vector.quantize_mx(
+                out=h_codes[u][:, cols].bitcast(FP8X4),
+                scales=h_scales[u][:, cols],
+                in_=h_grouped[u][:, 4 * cols.start : 4 * cols.stop],
+            )
 
-        def second_matmul(slab):
+        def second_matmul(slab, g, c):
             b, kt = divmod(slab, 2)
+            u = 2 * b + c
             slots = slice(128 * kt, 128 * kt + 128)
-            for g in range(2):
-                bank = psum.tile([P, 512], F32, name="agg_bank", tag="bank")
-                agg_bank[(slab, g)] = bank
-                cols = slice(512 * g, 512 * g + 512)
-                for c in range(2):
-                    u = 2 * b + c
-                    nc.tensor.matmul_mx(
-                        out=bank[:],
-                        lhsT=route_codes[u][:, slots].bitcast(FP8X4),
-                        lhsT_scale=route_scales[u][:, slots],
-                        rhs=h_codes[u][:, cols].bitcast(FP8X4),
-                        rhs_scale=h_scales[u][:, cols],
-                        start=(c == 0),
-                        stop=(c == 1),
-                    )
+            cols = slice(512 * g, 512 * g + 512)
+            if c == 0:
+                agg_bank[(slab, g)] = psum.tile([P, 512], F32, name="agg_bank", tag="bank")
+            nc.tensor.matmul_mx(
+                out=agg_bank[(slab, g)][:],
+                lhsT=route_codes[u][:, slots].bitcast(FP8X4),
+                lhsT_scale=route_scales[u][:, slots],
+                rhs=h_codes[u][:, cols].bitcast(FP8X4),
+                rhs_scale=h_scales[u][:, cols],
+                start=(c == 0),
+                stop=(c == 1),
+            )
 
         def copy_agg(slab, g, engine):
             if slab not in agg_sb:
                 agg_sb[slab] = work.tile([P, 1024], F32, name="agg_sb", tag="agg_sb", bufs=4)
             copy_on(engine, agg_sb[slab][:, 512 * g : 512 * g + 512], agg_bank[(slab, g)][:])
 
-        def store(slab):
+        def store(slab, halves=(0, 1)):
             b, kt = divmod(slab, 2)
-            rows = out[b, 128 * kt : 128 * kt + 128, :]
-            if slab >= FINE_STORES_FROM:
-                for g in range(2):
-                    cols = slice(512 * g, 512 * g + 512)
-                    nc.sync.dma_start(out=rows[:, cols], in_=agg_sb[slab][:, cols])
-            else:
-                nc.sync.dma_start(out=rows, in_=agg_sb[slab][:])
-            progress["stored"] = progress["stored"] + 1
+            cols = slice(512 * halves[0], 512 * halves[-1] + 512)
+            nc.sync.dma_start(out=out[b, 128 * kt : 128 * kt + 128, cols], in_=agg_sb[slab][:, cols])
 
         regroup_list = [("copy", 0, 0), ("copy", 0, 1)]
         for u in range(1, UNITS):
             regroup_list.extend([("copy", u, 0), ("quantise", u - 1, 0), ("copy", u, 1)])
-        regroup_list.append(("quantise", UNITS - 1, 0))
         scalar_regroups = ((0, 1), (1, 0))
 
         def regroup_items(n):
@@ -252,60 +254,84 @@ def tile_instrumentspecificslotmemory_pa_t_kernel(tc, H, Wr, br, out):
                         quantise_h(u)
                         progress["h_quantised"] = u
 
-        def is_unit(u):
-            return 0 <= u < UNITS
-
         waiting = []
-        s = 0
-        while progress["stored"] < SLABS:
-            light = s < UNITS and s % LIGHT_EVERY == 0
-            items = 2 if light else 3
-            if is_unit(s):
-                transpose_h(s, 0)
-            for slab, g in waiting:
-                copy_agg(slab, g, "scalar")
-            for slab in sorted(set([bank[0] for bank in waiting])):
+
+        def empty_slabs():
+            for slab in waiting:
+                for g in range(2):
+                    copy_agg(slab, g, "scalar")
                 store(slab)
-            waiting = []
-            if is_unit(s):
-                copy_ht(s, 0, 0, "scalar")
-                copy_ht(s, 0, 1, "scalar")
-            if is_unit(s - 1):
+            waiting.clear()
+
+        def whole_slab(slab):
+            for g in range(2):
+                for c in range(2):
+                    second_matmul(slab, g, c)
+            waiting.append(slab)
+
+        for s in range(UNITS):
+            items = 1 if s == 0 else (0 if s == UNITS - 1 else ITEMS)
+            order = [(0, 0), (1, 0), (0, 1), (1, 1)]
+            for jp, g in order[0:2]:
+                transpose_h(s, jp, g)
+            empty_slabs()
+            for jp, g in order[0:2]:
+                copy_ht(s, jp, g, "scalar")
+            if s >= 1:
                 quantise_ht(s - 1)
-            if is_unit(s - 2):
+            if s >= 2:
                 transpose_route(s - 2)
-            if is_unit(s):
-                transpose_h(s, 1)
-                progress["transposed"] = s
+            for jp, g in order[2:4]:
+                transpose_h(s, jp, g)
+            progress["transposed"] = s
             if s == 0:
                 regroup_items(1)
-                prepare_weights()
-            if is_unit(s - 2):
+            if s >= 2:
                 copy_route(s - 2)
             regroup_items((items + 1) // 2)
-            if is_unit(s):
-                copy_ht(s, 1, 0, "vector" if light else "scalar")
-                copy_ht(s, 1, 1, "vector" if light else "scalar")
-            if is_unit(s - 1):
+            for jp, g in order[2:4]:
+                copy_ht(s, jp, g, "vector" if s == 0 else "scalar")
+            if s == 0:
+                prepare_weights()
+            if s >= 1:
                 first_matmul(s - 1)
-            multiplied_here = []
-            while progress["multiplied"] < SLABS and len(multiplied_here) < (2 if s > UNITS else 1):
-                second_unit = 2 * (progress["multiplied"] // 2) + 1
-                if second_unit + 3 > s or progress["h_quantised"] < second_unit:
-                    break
-                second_matmul(progress["multiplied"])
-                multiplied_here.append(progress["multiplied"])
-                progress["multiplied"] = progress["multiplied"] + 1
+            slab = progress["multiplied"]
+            if 2 * (slab // 2) + 4 <= s and progress["h_quantised"] >= 2 * (slab // 2) + 1:
+                whole_slab(slab)
+                progress["multiplied"] = slab + 1
             regroup_items(items // 2)
-            if is_unit(s - 2):
+            if s >= 2:
                 quantise_route(s - 2)
-            for slab in multiplied_here:
-                if s >= UNITS:
-                    copy_agg(slab, 1, "vector")
-                    waiting.append((slab, 0))
-                else:
-                    waiting.extend([(slab, 0), (slab, 1)])
-            if is_unit(s - 1):
+            if s >= 1:
                 sigmoid(s - 1)
             load_up_to(min(progress["transposed"], progress["regrouped"]) + 1 + H_BUFS)
-            s = s + 1
+
+        last = UNITS - 1
+        assert progress["multiplied"] == SLABS - 4
+        quantise_ht(last)
+        transpose_route(last - 1)
+        empty_slabs()
+        first_matmul(last)
+        whole_slab(SLABS - 4)
+        copy_route(last - 1)
+        while progress["regroup"] < len(regroup_list) - 1:
+            regroup_items(1)
+        quantise_route(last - 1)
+        sigmoid(last)
+        empty_slabs()
+        transpose_route(last)
+        whole_slab(SLABS - 3)
+        copy_route(last)
+        empty_slabs()
+        for slab in (SLABS - 2, SLABS - 1):
+            for g in range(2):
+                second_matmul(slab, g, 0)
+        quantise_h(last, (0,))
+        regroup_items(1)
+        quantise_route(last)
+        quantise_h(last, (1,))
+        for g in range(2):
+            for slab in (SLABS - 2, SLABS - 1):
+                second_matmul(slab, g, 1)
+                copy_agg(slab, g, "vector" if g == 1 and slab == SLABS - 1 else "scalar")
+                store(slab, (g,))

@@ -193,9 +193,9 @@ def tile_instrumentspecificslotmemory_pa_t_kernel(tc, H, Wr, br, out):
         def regroup_h(u, g, engine):
             if g == 0:
                 h_grouped[u] = work.tile([P, 4096], BF16, name="h_grouped", tag="h_grouped", bufs=3, align_bytes=64)
-            dst = h_grouped[u][:].rearrange("p (run i j) -> p run j i", i=4, j=4)
-            src = h_sb[u][:].rearrange("p (j run i) -> p run j i", j=4, i=4)
-            runs = slice(128 * g, 128 * g + 128)
+            dst = h_grouped[u][:].rearrange("p (run i j) -> p run j i", i=8, j=4)
+            src = h_sb[u][:].rearrange("p (j run i) -> p run j i", j=4, i=8)
+            runs = slice(64 * g, 64 * g + 64)
             copy_on(engine, dst[:, runs], src[:, runs])
 
         def quantise_h(u, halves=(0, 1)):

@@ -274,13 +274,16 @@ def tile_instrumentspecificslotmemory_pa_t_kernel(tc, H, Wr, br, out):
             order = [(0, 0), (1, 0), (0, 1), (1, 1)]
             for jp, g in order[0:2]:
                 transpose_h(s, jp, g)
-            empty_slabs()
             for jp, g in order[0:2]:
                 copy_ht(s, jp, g, "scalar")
             if s >= 1:
                 quantise_ht(s - 1)
             if s >= 2:
                 transpose_route(s - 2)
+            slab = progress["multiplied"]
+            if 2 * (slab // 2) + 4 <= s and progress["h_quantised"] >= 2 * (slab // 2) + 1:
+                whole_slab(slab)
+                progress["multiplied"] = slab + 1
             for jp, g in order[2:4]:
                 transpose_h(s, jp, g)
             progress["transposed"] = s
@@ -288,20 +291,17 @@ def tile_instrumentspecificslotmemory_pa_t_kernel(tc, H, Wr, br, out):
                 regroup_items(1)
             if s >= 2:
                 copy_route(s - 2)
-            regroup_items((items + 1) // 2)
+            regroup_items(min(items, 2))
+            if s >= 2:
+                quantise_route(s - 2)
+            empty_slabs()
             for jp, g in order[2:4]:
                 copy_ht(s, jp, g, "vector" if s == 0 else "scalar")
             if s == 0:
                 prepare_weights()
             if s >= 1:
                 first_matmul(s - 1)
-            slab = progress["multiplied"]
-            if 2 * (slab // 2) + 4 <= s and progress["h_quantised"] >= 2 * (slab // 2) + 1:
-                whole_slab(slab)
-                progress["multiplied"] = slab + 1
-            regroup_items(items // 2)
-            if s >= 2:
-                quantise_route(s - 2)
+            regroup_items(items - min(items, 2))
             if s >= 1:
                 sigmoid(s - 1)
             load_up_to(min(progress["transposed"], progress["regrouped"]) + 1 + H_BUFS)

@@ -18,7 +18,6 @@ FLOPS = 2 * 2 * B * T * D * K
 
 H_BUFS = 8
 CODE_BUFS = 6
-ITEMS = 3
 
 
 def tile_instrumentspecificslotmemory_pa_t_kernel(tc, H, Wr, br, out):
@@ -190,12 +189,12 @@ def tile_instrumentspecificslotmemory_pa_t_kernel(tc, H, Wr, br, out):
                 out=route_codes[u][:].bitcast(FP8X4), scales=route_scales[u][:], in_=route_grouped[u][:]
             )
 
-        def regroup_h(u, g, engine):
-            if g == 0:
+        def regroup_h(u, halves, engine):
+            if u not in h_grouped:
                 h_grouped[u] = work.tile([P, 4096], BF16, name="h_grouped", tag="h_grouped", bufs=3, align_bytes=64)
             dst = h_grouped[u][:].rearrange("p (run i j) -> p run j i", i=8, j=4)
             src = h_sb[u][:].rearrange("p (j run i) -> p run j i", j=4, i=8)
-            runs = slice(64 * g, 64 * g + 64)
+            runs = slice(64 * halves[0], 64 * halves[-1] + 64)
             copy_on(engine, dst[:, runs], src[:, runs])
 
         def quantise_h(u, halves=(0, 1)):
@@ -236,19 +235,20 @@ def tile_instrumentspecificslotmemory_pa_t_kernel(tc, H, Wr, br, out):
             cols = slice(512 * halves[0], 512 * halves[-1] + 512)
             nc.sync.dma_start(out=out[b, 128 * kt : 128 * kt + 128, cols], in_=agg_sb[slab][:, cols])
 
-        regroup_list = [("copy", 0, 0), ("copy", 0, 1)]
-        for u in range(1, UNITS):
-            regroup_list.extend([("copy", u, 0), ("quantise", u - 1, 0), ("copy", u, 1)])
-        scalar_regroups = ((0, 1), (1, 0))
+        regroup_list = [("copy", 0, (0,)), ("copy", 0, (1,)), ("copy", 1, (0,)), ("quantise", 0, None), ("copy", 1, (1,))]
+        for u in range(2, UNITS - 1):
+            regroup_list.extend([("copy", u, (0, 1)), ("quantise", u - 1, None)])
+        regroup_list.extend([("copy", UNITS - 1, (0,)), ("quantise", UNITS - 2, None), ("copy", UNITS - 1, (1,))])
+        scalar_regroups = ((0, (1,)), (1, (0,)))
 
         def regroup_items(n):
             for i in range(n):
                 if progress["regroup"] < len(regroup_list):
-                    kind, u, g = regroup_list[progress["regroup"]]
+                    kind, u, halves = regroup_list[progress["regroup"]]
                     progress["regroup"] = progress["regroup"] + 1
                     if kind == "copy":
-                        regroup_h(u, g, "scalar" if (u, g) in scalar_regroups else "vector")
-                        if g == 1:
+                        regroup_h(u, halves, "scalar" if (u, halves) in scalar_regroups else "vector")
+                        if halves[-1] == 1:
                             progress["regrouped"] = u
                     else:
                         quantise_h(u)
@@ -270,7 +270,7 @@ def tile_instrumentspecificslotmemory_pa_t_kernel(tc, H, Wr, br, out):
             waiting.append(slab)
 
         for s in range(UNITS):
-            items = 1 if s == 0 else (0 if s == UNITS - 1 else ITEMS)
+            items = (1, 3)[s] if s < 2 else (1 if s == UNITS - 1 else 2)
             order = [(0, 0), (1, 0), (0, 1), (1, 1)]
             for jp, g in order[0:2]:
                 transpose_h(s, jp, g)
@@ -291,7 +291,7 @@ def tile_instrumentspecificslotmemory_pa_t_kernel(tc, H, Wr, br, out):
                 regroup_items(1)
             if s >= 2:
                 copy_route(s - 2)
-            regroup_items(min(items, 2))
+            regroup_items((items + 1) // 2)
             if s >= 2:
                 quantise_route(s - 2)
             empty_slabs()
@@ -301,7 +301,7 @@ def tile_instrumentspecificslotmemory_pa_t_kernel(tc, H, Wr, br, out):
                 prepare_weights()
             if s >= 1:
                 first_matmul(s - 1)
-            regroup_items(items - min(items, 2))
+            regroup_items(items // 2)
             if s >= 1:
                 sigmoid(s - 1)
             load_up_to(min(progress["transposed"], progress["regrouped"]) + 1 + H_BUFS)
@@ -309,20 +309,22 @@ def tile_instrumentspecificslotmemory_pa_t_kernel(tc, H, Wr, br, out):
         last = UNITS - 1
         assert progress["multiplied"] == SLABS - 4
         quantise_ht(last)
+        whole_slab(SLABS - 4)
         transpose_route(last - 1)
         empty_slabs()
-        first_matmul(last)
-        whole_slab(SLABS - 4)
         copy_route(last - 1)
+        first_matmul(last)
+        whole_slab(SLABS - 3)
+        waiting.clear()
         while progress["regroup"] < len(regroup_list) - 1:
             regroup_items(1)
         quantise_route(last - 1)
         sigmoid(last)
-        empty_slabs()
         transpose_route(last)
-        whole_slab(SLABS - 3)
+        copy_agg(SLABS - 3, 0, "scalar")
         copy_route(last)
-        empty_slabs()
+        copy_agg(SLABS - 3, 1, "scalar")
+        store(SLABS - 3)
         for slab in (SLABS - 2, SLABS - 1):
             for g in range(2):
                 second_matmul(slab, g, 0)

@@ -97,7 +97,7 @@ def tile_instrumentspecificslotmemory_pa_t_kernel(tc, H, Wr, br, out):
                     for kt in range(2):
                         lo = 512 * kt + 256 * g + 128 * blk
                         nc.tensor.transpose(bank[:, blk, kt, :], words[:, lo : lo + 128], ident_f32[:])
-                nc.vector.tensor_copy(
+                nc.scalar.copy(
                     out=grouped[:, g, :, :].rearrange("p (kt k) blk -> p kt k blk", kt=2),
                     in_=bank[:].rearrange("p blk kt k -> p kt k blk"),
                 )
@@ -115,14 +115,13 @@ def tile_instrumentspecificslotmemory_pa_t_kernel(tc, H, Wr, br, out):
                     lo = 512 * (2 * jp + jl) + 256 * g + 128 * blk
                     nc.tensor.transpose(bank[:, jl, blk, :], words[:, lo : lo + 128], ident_f32[:])
 
-        def copy_ht(u, jp, g, engine):
+        def copy_ht(u, jp, g):
             if u not in ht_grouped:
                 ht_grouped[u] = work.tile([P, 4096], BF16, name="ht_grouped", tag="ht_grouped", align_bytes=64)
             grouped = ht_grouped[u][:].bitcast(F32).rearrange("p (g col blk) -> p g col blk", g=2, blk=2)
-            copy_on(
-                engine,
-                grouped[:, g, 256 * jp : 256 * jp + 256, :].rearrange("p (jl q) blk -> p jl q blk", jl=2),
-                ht_bank[(u, g, jp)][:].rearrange("p jl blk q -> p jl q blk"),
+            nc.scalar.copy(
+                out=grouped[:, g, 256 * jp : 256 * jp + 256, :].rearrange("p (jl q) blk -> p jl q blk", jl=2),
+                in_=ht_bank[(u, g, jp)][:].rearrange("p jl blk q -> p jl q blk"),
             )
 
         def quantise_ht(u):
@@ -239,7 +238,7 @@ def tile_instrumentspecificslotmemory_pa_t_kernel(tc, H, Wr, br, out):
         for u in range(2, UNITS - 1):
             regroup_list.extend([("copy", u, (0, 1)), ("quantise", u - 1, None)])
         regroup_list.extend([("copy", UNITS - 1, (0,)), ("quantise", UNITS - 2, None), ("copy", UNITS - 1, (1,))])
-        scalar_regroups = ((0, (1,)), (1, (0,)))
+        scalar_regroups = ((1, (1,)),)
 
         def regroup_items(n):
             for i in range(n):
@@ -270,12 +269,11 @@ def tile_instrumentspecificslotmemory_pa_t_kernel(tc, H, Wr, br, out):
             waiting.append(slab)
 
         for s in range(UNITS):
-            items = (1, 3)[s] if s < 2 else (1 if s == UNITS - 1 else 2)
+            items = 1 if s in (0, UNITS - 1) else 2
             order = [(0, 0), (1, 0), (0, 1), (1, 1)]
             for jp, g in order[0:2]:
                 transpose_h(s, jp, g)
-            for jp, g in order[0:2]:
-                copy_ht(s, jp, g, "scalar")
+                copy_ht(s, jp, g)
             if s >= 1:
                 quantise_ht(s - 1)
             if s >= 2:
@@ -288,7 +286,7 @@ def tile_instrumentspecificslotmemory_pa_t_kernel(tc, H, Wr, br, out):
                 transpose_h(s, jp, g)
             progress["transposed"] = s
             if s == 0:
-                regroup_items(1)
+                regroup_items(2)
             if s >= 2:
                 copy_route(s - 2)
             regroup_items((items + 1) // 2)
@@ -296,7 +294,7 @@ def tile_instrumentspecificslotmemory_pa_t_kernel(tc, H, Wr, br, out):
                 quantise_route(s - 2)
             empty_slabs()
             for jp, g in order[2:4]:
-                copy_ht(s, jp, g, "vector" if s == 0 else "scalar")
+                copy_ht(s, jp, g)
             if s == 0:
                 prepare_weights()
             if s >= 1:

@@ -188,13 +188,13 @@ def tile_instrumentspecificslotmemory_pa_t_kernel(tc, H, Wr, br, out):
                 out=route_codes[u][:].bitcast(FP8X4), scales=route_scales[u][:], in_=route_grouped[u][:]
             )
 
-        def regroup_h(u, halves, engine):
+        def regroup_h(u, halves):
             if u not in h_grouped:
                 h_grouped[u] = work.tile([P, 4096], BF16, name="h_grouped", tag="h_grouped", bufs=3, align_bytes=64)
             dst = h_grouped[u][:].rearrange("p (run i j) -> p run j i", i=8, j=4)
             src = h_sb[u][:].rearrange("p (j run i) -> p run j i", j=4, i=8)
             runs = slice(64 * halves[0], 64 * halves[-1] + 64)
-            copy_on(engine, dst[:, runs], src[:, runs])
+            nc.vector.tensor_copy(out=dst[:, runs], in_=src[:, runs])
 
         def quantise_h(u, halves=(0, 1)):
             if u not in h_codes:
@@ -238,7 +238,6 @@ def tile_instrumentspecificslotmemory_pa_t_kernel(tc, H, Wr, br, out):
         for u in range(2, UNITS - 1):
             regroup_list.extend([("copy", u, (0, 1)), ("quantise", u - 1, None)])
         regroup_list.extend([("copy", UNITS - 1, (0,)), ("quantise", UNITS - 2, None), ("copy", UNITS - 1, (1,))])
-        scalar_regroups = ((1, (1,)),)
 
         def regroup_items(n):
             for i in range(n):
@@ -246,7 +245,7 @@ def tile_instrumentspecificslotmemory_pa_t_kernel(tc, H, Wr, br, out):
                     kind, u, halves = regroup_list[progress["regroup"]]
                     progress["regroup"] = progress["regroup"] + 1
                     if kind == "copy":
-                        regroup_h(u, halves, "scalar" if (u, halves) in scalar_regroups else "vector")
+                        regroup_h(u, halves)
                         if halves[-1] == 1:
                             progress["regrouped"] = u
                     else:

@@ -18,6 +18,9 @@ FLOPS = 2 * 2 * B * T * D * K
 
 H_BUFS = 8
 CODE_BUFS = 6
+LOADED_IN_PIECES = (0, 1)
+WARM_FIRST = 12
+WARM_BANK = 4
 
 
 def tile_instrumentspecificslotmemory_pa_t_kernel(tc, H, Wr, br, out):
@@ -45,26 +48,37 @@ def tile_instrumentspecificslotmemory_pa_t_kernel(tc, H, Wr, br, out):
 
         w_sb = const.tile([P, 2 * D], BF16, name="w_sb")
 
+        def load_weights():
+            nc.sync.dma_start(
+                out=w_sb[:].rearrange("p (kt d) -> p kt d", kt=2),
+                in_=Wr.rearrange("(kt p) d -> p kt d", p=P),
+            )
+
+        def h_start(u, j, g):
+            return 2048 * g + 512 * j if u in LOADED_IN_PIECES else 1024 * j + 512 * g
+
+        def load_piece(u, rows, g, j, n):
+            lo = h_start(u, j, g)
+            nc.sync.dma_start(
+                out=h_sb[u][:, lo : lo + 512 * n].rearrange("p (j d) -> p j d", j=n),
+                in_=rows[:, j : j + n, 512 * g : 512 * g + 512],
+            )
+
         def load(u):
             b, c = divmod(u, 2)
             h_sb[u] = h_pool.tile([P, 4 * D], BF16, name="h_sb", tag="h_sb")
             rows = H[b, 512 * c : 512 * c + 512, :].rearrange("(p j) d -> p j d", j=4)
-            dst = h_sb[u][:].rearrange("p (j d) -> p j d", j=4)
             if u == 0:
                 for g in range(2):
                     for jp in range(2):
-                        piece = (slice(None), slice(2 * jp, 2 * jp + 2), slice(512 * g, 512 * g + 512))
-                        nc.sync.dma_start(out=dst[piece], in_=rows[piece])
-                nc.sync.dma_start(
-                    out=w_sb[:].rearrange("p (kt d) -> p kt d", kt=2),
-                    in_=Wr.rearrange("(kt p) d -> p kt d", p=P),
-                )
+                        load_piece(u, rows, g, 2 * jp, 2)
             elif u == 1:
                 for g in range(2):
-                    piece = (slice(None), slice(None), slice(512 * g, 512 * g + 512))
-                    nc.sync.dma_start(out=dst[piece], in_=rows[piece])
+                    load_piece(u, rows, g, 0, 4)
+                    if g == 0:
+                        load_weights()
             else:
-                nc.sync.dma_start(out=dst, in_=rows)
+                nc.sync.dma_start(out=h_sb[u][:].rearrange("p (j d) -> p j d", j=4), in_=rows)
 
         def load_up_to(n):
             while progress["loaded"] < min(n, UNITS):
@@ -78,6 +92,15 @@ def tile_instrumentspecificslotmemory_pa_t_kernel(tc, H, Wr, br, out):
         warm_out = const.tile([P, 1], F32, name="warm_out")
         nc.vector.memset(warm_in[:], 0.0)
         nc.scalar.activation(out=warm_out[:], in_=warm_in[:], func=ACT.Sigmoid)
+        zeros = const.tile([P, P], BF16, name="zeros")
+        nc.vector.memset(zeros[:], 0.0)
+        warm_bank = psum.tile([P, 512], F32, name="warm_bank", tag="bank")
+
+        def warm_up(n):
+            for i in range(n):
+                nc.tensor.matmul(out=warm_bank[:, 0:P], lhsT=zeros[:], rhs=zeros[:], start=True, stop=True)
+
+        warm_up(WARM_FIRST)
         load_up_to(H_BUFS)
         ident_f32 = const.tile([P, P], F32, name="ident_f32")
         make_identity(nc, ident_f32[:])
@@ -88,7 +111,7 @@ def tile_instrumentspecificslotmemory_pa_t_kernel(tc, H, Wr, br, out):
         w_codes = const.tile([P, 512], U32, name="w_codes", align_bytes=64)
         w_scales = const.tile([P, 512], U8, name="w_scales", align_bytes=64)
 
-        def prepare_weights():
+        def turn_weights():
             words = w_sb[:].bitcast(F32)
             grouped = w_grouped[:].bitcast(F32).rearrange("p (g k blk) -> p g k blk", g=2, blk=2)
             for g in range(2):
@@ -103,7 +126,9 @@ def tile_instrumentspecificslotmemory_pa_t_kernel(tc, H, Wr, br, out):
                 )
             bank = psum.tile([P, 4, 256], BF16, name="bias_bank", tag="bank")
             nc.tensor.transpose(bank[:, 0, 0:P], bias_rows[:], ident_bf16[:])
-            nc.vector.tensor_copy(out=bias[:], in_=bank[:, 0, 0:2])
+            nc.scalar.copy(out=bias[:], in_=bank[:, 0, 0:2])
+
+        def quantise_weights():
             nc.vector.quantize_mx(out=w_codes[:].bitcast(FP8X4), scales=w_scales[:], in_=w_grouped[:])
 
         def transpose_h(u, jp, g):
@@ -112,7 +137,7 @@ def tile_instrumentspecificslotmemory_pa_t_kernel(tc, H, Wr, br, out):
             ht_bank[(u, g, jp)] = bank
             for jl in range(2):
                 for blk in range(2):
-                    lo = 512 * (2 * jp + jl) + 256 * g + 128 * blk
+                    lo = h_start(u, 2 * jp + jl, g) // 2 + 128 * blk
                     nc.tensor.transpose(bank[:, jl, blk, :], words[:, lo : lo + 128], ident_f32[:])
 
         def copy_ht(u, jp, g):
@@ -171,30 +196,38 @@ def tile_instrumentspecificslotmemory_pa_t_kernel(tc, H, Wr, br, out):
                     )
 
         def copy_route(u):
-            route_grouped[u] = work.tile([P, 1024], BF16, name="route_grouped", tag="route_grouped", align_bytes=64)
-            nc.scalar.copy(
-                out=route_grouped[u][:].bitcast(F32).rearrange("p (k jp) -> p k jp", jp=2),
-                in_=route_bank[u][:].rearrange("p jp k -> p k jp"),
-            )
+            b, c = divmod(u, 2)
+            if c == 0:
+                route_grouped[b] = work.tile([P, 2048], BF16, name="route_grouped", tag="route_grouped", align_bytes=64)
+            grouped = route_grouped[b][:].bitcast(F32).rearrange("p (c k jp) -> p c k jp", c=2, jp=2)
+            nc.scalar.copy(out=grouped[:, c], in_=route_bank[u][:].rearrange("p jp k -> p k jp"))
 
-        def quantise_route(u):
-            route_codes[u] = work.tile(
-                [P, 256], U32, name="route_codes", tag="route_codes", bufs=CODE_BUFS, align_bytes=64
-            )
-            route_scales[u] = work.tile(
-                [P, 256], U8, name="route_scales", tag="route_scales", bufs=CODE_BUFS, align_bytes=64
-            )
+        def quantise_route(b, units=(0, 1)):
+            if b not in route_codes:
+                route_codes[b] = work.tile(
+                    [P, 512], U32, name="route_codes", tag="route_codes", bufs=CODE_BUFS // 2, align_bytes=64
+                )
+                route_scales[b] = work.tile(
+                    [P, 512], U8, name="route_scales", tag="route_scales", bufs=CODE_BUFS // 2, align_bytes=64
+                )
+            cols = slice(256 * units[0], 256 * units[-1] + 256)
             nc.vector.quantize_mx(
-                out=route_codes[u][:].bitcast(FP8X4), scales=route_scales[u][:], in_=route_grouped[u][:]
+                out=route_codes[b][:, cols].bitcast(FP8X4),
+                scales=route_scales[b][:, cols],
+                in_=route_grouped[b][:, 4 * cols.start : 4 * cols.stop],
             )
 
         def regroup_h(u, halves):
             if u not in h_grouped:
                 h_grouped[u] = work.tile([P, 4096], BF16, name="h_grouped", tag="h_grouped", bufs=3, align_bytes=64)
             dst = h_grouped[u][:].rearrange("p (run i j) -> p run j i", i=8, j=4)
-            src = h_sb[u][:].rearrange("p (j run i) -> p run j i", j=4, i=8)
             runs = slice(64 * halves[0], 64 * halves[-1] + 64)
-            nc.vector.tensor_copy(out=dst[:, runs], in_=src[:, runs])
+            if u in LOADED_IN_PIECES:
+                half = h_sb[u][:, 2048 * halves[0] : 2048 * halves[0] + 2048]
+                src = half.rearrange("p (j run i) -> p run j i", j=4, i=8)
+            else:
+                src = h_sb[u][:].rearrange("p (j run i) -> p run j i", j=4, i=8)[:, runs]
+            nc.vector.tensor_copy(out=dst[:, runs], in_=src)
 
         def quantise_h(u, halves=(0, 1)):
             if u not in h_codes:
@@ -210,14 +243,14 @@ def tile_instrumentspecificslotmemory_pa_t_kernel(tc, H, Wr, br, out):
         def second_matmul(slab, g, c):
             b, kt = divmod(slab, 2)
             u = 2 * b + c
-            slots = slice(128 * kt, 128 * kt + 128)
+            slots = slice(256 * c + 128 * kt, 256 * c + 128 * kt + 128)
             cols = slice(512 * g, 512 * g + 512)
             if c == 0:
                 agg_bank[(slab, g)] = psum.tile([P, 512], F32, name="agg_bank", tag="bank")
             nc.tensor.matmul_mx(
                 out=agg_bank[(slab, g)][:],
-                lhsT=route_codes[u][:, slots].bitcast(FP8X4),
-                lhsT_scale=route_scales[u][:, slots],
+                lhsT=route_codes[b][:, slots].bitcast(FP8X4),
+                lhsT_scale=route_scales[b][:, slots],
                 rhs=h_codes[u][:, cols].bitcast(FP8X4),
                 rhs_scale=h_scales[u][:, cols],
                 start=(c == 0),
@@ -268,13 +301,23 @@ def tile_instrumentspecificslotmemory_pa_t_kernel(tc, H, Wr, br, out):
             waiting.append(slab)
 
         for s in range(UNITS):
-            items = 1 if s in (0, UNITS - 1) else 2
             order = [(0, 0), (1, 0), (0, 1), (1, 1)]
+            if s == 1:
+                turn_weights()
             for jp, g in order[0:2]:
                 transpose_h(s, jp, g)
                 copy_ht(s, jp, g)
+                if s == 0:
+                    warm_up(WARM_BANK)
+            if s == 0:
+                regroup_items(2)
+            if s == 1:
+                regroup_items(1)
             if s >= 1:
                 quantise_ht(s - 1)
+            if s == 1:
+                regroup_items(1)
+                quantise_weights()
             if s >= 2:
                 transpose_route(s - 2)
             slab = progress["multiplied"]
@@ -283,22 +326,21 @@ def tile_instrumentspecificslotmemory_pa_t_kernel(tc, H, Wr, br, out):
                 progress["multiplied"] = slab + 1
             for jp, g in order[2:4]:
                 transpose_h(s, jp, g)
+                if s == 0:
+                    warm_up(WARM_BANK)
             progress["transposed"] = s
-            if s == 0:
-                regroup_items(2)
             if s >= 2:
                 copy_route(s - 2)
-            regroup_items((items + 1) // 2)
-            if s >= 2:
-                quantise_route(s - 2)
+                regroup_items(1)
+            if s >= 3 and s % 2 == 1:
+                quantise_route((s - 3) // 2)
             empty_slabs()
             for jp, g in order[2:4]:
                 copy_ht(s, jp, g)
-            if s == 0:
-                prepare_weights()
             if s >= 1:
                 first_matmul(s - 1)
-            regroup_items(items // 2)
+            if 1 <= s < UNITS - 1:
+                regroup_items(1)
             if s >= 1:
                 sigmoid(s - 1)
             load_up_to(min(progress["transposed"], progress["regrouped"]) + 1 + H_BUFS)
@@ -315,7 +357,7 @@ def tile_instrumentspecificslotmemory_pa_t_kernel(tc, H, Wr, br, out):
         waiting.clear()
         while progress["regroup"] < len(regroup_list) - 1:
             regroup_items(1)
-        quantise_route(last - 1)
+        quantise_route(last // 2, (0,))
         sigmoid(last)
         transpose_route(last)
         copy_agg(SLABS - 3, 0, "scalar")
@@ -327,7 +369,7 @@ def tile_instrumentspecificslotmemory_pa_t_kernel(tc, H, Wr, br, out):
                 second_matmul(slab, g, 0)
         quantise_h(last, (0,))
         regroup_items(1)
-        quantise_route(last)
+        quantise_route(last // 2, (1,))
         quantise_h(last, (1,))
         for g in range(2):
             for slab in (SLABS - 2, SLABS - 1):

@@ -94,6 +94,8 @@ def tile_instrumentspecificslotmemory_pa_t_kernel(tc, H, Wr, br, out):
         nc.scalar.activation(out=warm_out[:], in_=warm_in[:], func=ACT.Sigmoid)
         zeros = const.tile([P, P], BF16, name="zeros")
         nc.vector.memset(zeros[:], 0.0)
+        wide_zeros = const.tile([P, 512], BF16, name="wide_zeros")
+        nc.gpsimd.memset(wide_zeros[:], 0.0)
         warm_bank = psum.tile([P, 512], F32, name="warm_bank", tag="bank")
 
         def warm_up(n):
@@ -156,9 +158,11 @@ def tile_instrumentspecificslotmemory_pa_t_kernel(tc, H, Wr, br, out):
                 out=ht_codes[u][:].bitcast(FP8X4), scales=ht_scales[u][:], in_=ht_grouped[u][:]
             )
 
-        def first_matmul(u):
+        def first_matmul(u, fill):
             for kt in range(2):
                 bank = psum.tile([P, 512], F32, name="sum_bank", tag="bank")
+                if fill and kt == 0:
+                    nc.tensor.matmul(out=bank[:], lhsT=zeros[:], rhs=wide_zeros[:], start=True, stop=True)
                 sum_bank[(u, kt)] = bank
                 for g in range(2):
                     slots = slice(256 * g + 128 * kt, 256 * g + 128 * kt + 128)
@@ -184,10 +188,15 @@ def tile_instrumentspecificslotmemory_pa_t_kernel(tc, H, Wr, br, out):
                     scale=1.0,
                 )
 
-        def transpose_route(u):
+        def transpose_route(u, fill):
             words = route_t[u][:].bitcast(F32)
             bank = psum.tile([P, 2, 256], F32, name="route_bank", tag="bank")
             route_bank[u] = bank
+            if fill:
+                for jp in range(2):
+                    nc.tensor.matmul(
+                        out=bank[:, jp, :], lhsT=zeros[:], rhs=wide_zeros[:, 0:256], start=True, stop=True
+                    )
             for kt in range(2):
                 for jp in range(2):
                     lo = 256 * kt + 128 * jp
@@ -319,7 +328,7 @@ def tile_instrumentspecificslotmemory_pa_t_kernel(tc, H, Wr, br, out):
                 regroup_items(1)
                 quantise_weights()
             if s >= 2:
-                transpose_route(s - 2)
+                transpose_route(s - 2, True)
             slab = progress["multiplied"]
             if 2 * (slab // 2) + 4 <= s and progress["h_quantised"] >= 2 * (slab // 2) + 1:
                 whole_slab(slab)
@@ -338,7 +347,7 @@ def tile_instrumentspecificslotmemory_pa_t_kernel(tc, H, Wr, br, out):
             for jp, g in order[2:4]:
                 copy_ht(s, jp, g)
             if s >= 1:
-                first_matmul(s - 1)
+                first_matmul(s - 1, True)
             if 1 <= s < UNITS - 1:
                 regroup_items(1)
             if s >= 1:
@@ -349,17 +358,17 @@ def tile_instrumentspecificslotmemory_pa_t_kernel(tc, H, Wr, br, out):
         assert progress["multiplied"] == SLABS - 4
         quantise_ht(last)
         whole_slab(SLABS - 4)
-        transpose_route(last - 1)
+        transpose_route(last - 1, False)
         empty_slabs()
         copy_route(last - 1)
-        first_matmul(last)
+        first_matmul(last, False)
         whole_slab(SLABS - 3)
         waiting.clear()
         while progress["regroup"] < len(regroup_list) - 1:
             regroup_items(1)
         quantise_route(last // 2, (0,))
         sigmoid(last)
-        transpose_route(last)
+        transpose_route(last, False)
         copy_agg(SLABS - 3, 0, "scalar")
         copy_route(last)
         copy_agg(SLABS - 3, 1, "scalar")
@@ -374,5 +383,5 @@ def tile_instrumentspecificslotmemory_pa_t_kernel(tc, H, Wr, br, out):
         for g in range(2):
             for slab in (SLABS - 2, SLABS - 1):
                 second_matmul(slab, g, 1)
-                copy_agg(slab, g, "vector" if g == 1 and slab == SLABS - 1 else "scalar")
+                copy_agg(slab, g, "vector" if slab == SLABS - 1 else "scalar")
                 store(slab, (g,))

from contextlib import ExitStack

import concourse.mybir as mybir
from concourse.masks import make_identity

F32 = mybir.dt.float32
BF16 = mybir.dt.bfloat16
U32 = mybir.dt.uint32
U8 = mybir.dt.uint8
FP8X4 = mybir.dt.float8_e4m3fn_x4
ACT = mybir.ActivationFunctionType

B, T, D, K = 8, 1024, 1024, 256
P = 128
UNITS = 2 * B
SLABS = 2 * B
FLOPS = 2 * 2 * B * T * D * K

H_BUFS = 8
CODE_BUFS = 6
LOADED_IN_PIECES = (0, 1)
WARM_FIRST = 12
WARM_BANK = 4


def tile_instrumentspecificslotmemory_pa_t_kernel(tc, H, Wr, br, out):
    nc = tc.nc
    with ExitStack() as ctx:
        const = ctx.enter_context(tc.tile_pool(name="const", bufs=1))
        h_pool = ctx.enter_context(tc.tile_pool(name="h_pool", bufs=H_BUFS))
        work = ctx.enter_context(tc.tile_pool(name="work", bufs=2))
        psum = ctx.enter_context(tc.psum_pool(name="psum", bufs=8))
        ctx.enter_context(tc.manual_schedule())

        h_sb, ht_bank, ht_grouped, ht_codes, ht_scales = {}, {}, {}, {}, {}
        sum_bank, route_t, route_bank, route_grouped, route_codes, route_scales = {}, {}, {}, {}, {}, {}
        h_grouped, h_codes, h_scales = {}, {}, {}
        agg_bank, agg_sb = {}, {}

        progress = {"loaded": 0, "regroup": 0, "transposed": -1, "regrouped": -1, "h_quantised": -1,
                    "multiplied": 0, "stored": 0}

        def copy_on(engine, dst, src):
            if engine == "scalar":
                nc.scalar.copy(out=dst, in_=src)
            else:
                nc.vector.tensor_copy(out=dst, in_=src)

        w_sb = const.tile([P, 2 * D], BF16, name="w_sb")

        def load_weights():
            nc.sync.dma_start(
                out=w_sb[:].rearrange("p (kt d) -> p kt d", kt=2),
                in_=Wr.rearrange("(kt p) d -> p kt d", p=P),
            )

        def h_start(u, j, g):
            return 2048 * g + 512 * j if u in LOADED_IN_PIECES else 1024 * j + 512 * g

        def load_piece(u, rows, g, j, n):
            lo = h_start(u, j, g)
            nc.sync.dma_start(
                out=h_sb[u][:, lo : lo + 512 * n].rearrange("p (j d) -> p j d", j=n),
                in_=rows[:, j : j + n, 512 * g : 512 * g + 512],
            )

        def load(u):
            b, c = divmod(u, 2)
            h_sb[u] = h_pool.tile([P, 4 * D], BF16, name="h_sb", tag="h_sb")
            rows = H[b, 512 * c : 512 * c + 512, :].rearrange("(p j) d -> p j d", j=4)
            if u == 0:
                for g in range(2):
                    for jp in range(2):
                        load_piece(u, rows, g, 2 * jp, 2)
            elif u == 1:
                for g in range(2):
                    load_piece(u, rows, g, 0, 4)
                    if g == 0:
                        load_weights()
            else:
                nc.sync.dma_start(out=h_sb[u][:].rearrange("p (j d) -> p j d", j=4), in_=rows)

        def load_up_to(n):
            while progress["loaded"] < min(n, UNITS):
                load(progress["loaded"])
                progress["loaded"] = progress["loaded"] + 1

        bias_rows = const.tile([P, P], BF16, name="bias_rows")
        nc.vector.memset(bias_rows[:], 0.0)
        nc.scalar.dma_start(out=bias_rows[0:2, :], in_=br.rearrange("(kt k) -> kt k", kt=2))
        warm_in = const.tile([P, 1], F32, name="warm_in")
        warm_out = const.tile([P, 1], F32, name="warm_out")
        nc.vector.memset(warm_in[:], 0.0)
        nc.scalar.activation(out=warm_out[:], in_=warm_in[:], func=ACT.Sigmoid)
        zeros = const.tile([P, P], BF16, name="zeros")
        nc.vector.memset(zeros[:], 0.0)
        wide_zeros = const.tile([P, 512], BF16, name="wide_zeros")
        nc.gpsimd.memset(wide_zeros[:], 0.0)
        warm_bank = psum.tile([P, 512], F32, name="warm_bank", tag="bank")

        def warm_up(n):
            for i in range(n):
                nc.tensor.matmul(out=warm_bank[:, 0:P], lhsT=zeros[:], rhs=zeros[:], start=True, stop=True)

        warm_up(WARM_FIRST)
        load_up_to(H_BUFS)
        ident_f32 = const.tile([P, P], F32, name="ident_f32")
        make_identity(nc, ident_f32[:])
        ident_bf16 = const.tile([P, P], BF16, name="ident_bf16")
        make_identity(nc, ident_bf16[:])
        bias = const.tile([P, 2], F32, name="bias")
        w_grouped = const.tile([P, 2048], BF16, name="w_grouped", align_bytes=64)
        w_codes = const.tile([P, 512], U32, name="w_codes", align_bytes=64)
        w_scales = const.tile([P, 512], U8, name="w_scales", align_bytes=64)

        def turn_weights():
            words = w_sb[:].bitcast(F32)
            grouped = w_grouped[:].bitcast(F32).rearrange("p (g k blk) -> p g k blk", g=2, blk=2)
            for g in range(2):
                bank = psum.tile([P, 2, 2, P], F32, name="w_bank", tag="bank")
                for blk in range(2):
                    for kt in range(2):
                        lo = 512 * kt + 256 * g + 128 * blk
                        nc.tensor.transpose(bank[:, blk, kt, :], words[:, lo : lo + 128], ident_f32[:])
                nc.scalar.copy(
                    out=grouped[:, g, :, :].rearrange("p (kt k) blk -> p kt k blk", kt=2),
                    in_=bank[:].rearrange("p blk kt k -> p kt k blk"),
                )
            bank = psum.tile([P, 4, 256], BF16, name="bias_bank", tag="bank")
            nc.tensor.transpose(bank[:, 0, 0:P], bias_rows[:], ident_bf16[:])
            nc.scalar.copy(out=bias[:], in_=bank[:, 0, 0:2])

        def quantise_weights():
            nc.vector.quantize_mx(out=w_codes[:].bitcast(FP8X4), scales=w_scales[:], in_=w_grouped[:])

        def transpose_h(u, jp, g):
            words = h_sb[u][:].bitcast(F32)
            bank = psum.tile([P, 2, 2, P], F32, name="ht_bank", tag="bank")
            ht_bank[(u, g, jp)] = bank
            for jl in range(2):
                for blk in range(2):
                    lo = h_start(u, 2 * jp + jl, g) // 2 + 128 * blk
                    nc.tensor.transpose(bank[:, jl, blk, :], words[:, lo : lo + 128], ident_f32[:])

        def copy_ht(u, jp, g):
            if u not in ht_grouped:
                ht_grouped[u] = work.tile([P, 4096], BF16, name="ht_grouped", tag="ht_grouped", align_bytes=64)
            grouped = ht_grouped[u][:].bitcast(F32).rearrange("p (g col blk) -> p g col blk", g=2, blk=2)
            nc.scalar.copy(
                out=grouped[:, g, 256 * jp : 256 * jp + 256, :].rearrange("p (jl q) blk -> p jl q blk", jl=2),
                in_=ht_bank[(u, g, jp)][:].rearrange("p jl blk q -> p jl q blk"),
            )

        def quantise_ht(u):
            ht_codes[u] = work.tile([P, 1024], U32, name="ht_codes", tag="ht_codes", align_bytes=64)
            ht_scales[u] = work.tile([P, 1024], U8, name="ht_scales", tag="ht_scales", align_bytes=64)
            nc.vector.quantize_mx(
                out=ht_codes[u][:].bitcast(FP8X4), scales=ht_scales[u][:], in_=ht_grouped[u][:]
            )

        def first_matmul(u, fill):
            for kt in range(2):
                bank = psum.tile([P, 512], F32, name="sum_bank", tag="bank")
                if fill and kt == 0:
                    nc.tensor.matmul(out=bank[:], lhsT=zeros[:], rhs=wide_zeros[:], start=True, stop=True)
                sum_bank[(u, kt)] = bank
                for g in range(2):
                    slots = slice(256 * g + 128 * kt, 256 * g + 128 * kt + 128)
                    cols = slice(512 * g, 512 * g + 512)
                    nc.tensor.matmul_mx(
                        out=bank[:],
                        lhsT=w_codes[:, slots].bitcast(FP8X4),
                        lhsT_scale=w_scales[:, slots],
                        rhs=ht_codes[u][:, cols].bitcast(FP8X4),
                        rhs_scale=ht_scales[u][:, cols],
                        start=(g == 0),
                        stop=(g == 1),
                    )

        def sigmoid(u):
            route_t[u] = work.tile([P, 1024], BF16, name="route_t", tag="route_t", bufs=3)
            for kt in range(2):
                nc.scalar.activation(
                    out=route_t[u][:, 512 * kt : 512 * kt + 512].rearrange("p (jp q e) -> p jp q e", jp=2, e=2),
                    in_=sum_bank[(u, kt)][:].rearrange("p (jp e q) -> p jp q e", jp=2, e=2),
                    func=ACT.Sigmoid,
                    bias=bias[:, kt : kt + 1],
                    scale=1.0,
                )

        def transpose_route(u, fill):
            words = route_t[u][:].bitcast(F32)
            bank = psum.tile([P, 2, 256], F32, name="route_bank", tag="bank")
            route_bank[u] = bank
            if fill:
                for jp in range(2):
                    nc.tensor.matmul(
                        out=bank[:, jp, :], lhsT=zeros[:], rhs=wide_zeros[:, 0:256], start=True, stop=True
                    )
            for kt in range(2):
                for jp in range(2):
                    lo = 256 * kt + 128 * jp
                    nc.tensor.transpose(
                        bank[:, jp, 128 * kt : 128 * kt + 128], words[:, lo : lo + 128], ident_f32[:]
                    )

        def copy_route(u):
            b, c = divmod(u, 2)
            if c == 0:
                route_grouped[b] = work.tile([P, 2048], BF16, name="route_grouped", tag="route_grouped", align_bytes=64)
            grouped = route_grouped[b][:].bitcast(F32).rearrange("p (c k jp) -> p c k jp", c=2, jp=2)
            nc.scalar.copy(out=grouped[:, c], in_=route_bank[u][:].rearrange("p jp k -> p k jp"))

        def quantise_route(b, units=(0, 1)):
            if b not in route_codes:
                route_codes[b] = work.tile(
                    [P, 512], U32, name="route_codes", tag="route_codes", bufs=CODE_BUFS // 2, align_bytes=64
                )
                route_scales[b] = work.tile(
                    [P, 512], U8, name="route_scales", tag="route_scales", bufs=CODE_BUFS // 2, align_bytes=64
                )
            cols = slice(256 * units[0], 256 * units[-1] + 256)
            nc.vector.quantize_mx(
                out=route_codes[b][:, cols].bitcast(FP8X4),
                scales=route_scales[b][:, cols],
                in_=route_grouped[b][:, 4 * cols.start : 4 * cols.stop],
            )

        def regroup_h(u, halves):
            if u not in h_grouped:
                h_grouped[u] = work.tile([P, 4096], BF16, name="h_grouped", tag="h_grouped", bufs=3, align_bytes=64)
            dst = h_grouped[u][:].rearrange("p (run i j) -> p run j i", i=8, j=4)
            runs = slice(64 * halves[0], 64 * halves[-1] + 64)
            if u in LOADED_IN_PIECES:
                half = h_sb[u][:, 2048 * halves[0] : 2048 * halves[0] + 2048]
                src = half.rearrange("p (j run i) -> p run j i", j=4, i=8)
            else:
                src = h_sb[u][:].rearrange("p (j run i) -> p run j i", j=4, i=8)[:, runs]
            nc.vector.tensor_copy(out=dst[:, runs], in_=src)

        def quantise_h(u, halves=(0, 1)):
            if u not in h_codes:
                h_codes[u] = work.tile([P, 1024], U32, name="h_codes", tag="h_codes", bufs=CODE_BUFS, align_bytes=64)
                h_scales[u] = work.tile([P, 1024], U8, name="h_scales", tag="h_scales", bufs=CODE_BUFS, align_bytes=64)
            cols = slice(512 * halves[0], 512 * halves[-1] + 512)
            nc.vector.quantize_mx(
                out=h_codes[u][:, cols].bitcast(FP8X4),
                scales=h_scales[u][:, cols],
                in_=h_grouped[u][:, 4 * cols.start : 4 * cols.stop],
            )

        def second_matmul(slab, g, c):
            b, kt = divmod(slab, 2)
            u = 2 * b + c
            slots = slice(256 * c + 128 * kt, 256 * c + 128 * kt + 128)
            cols = slice(512 * g, 512 * g + 512)
            if c == 0:
                agg_bank[(slab, g)] = psum.tile([P, 512], F32, name="agg_bank", tag="bank")
            nc.tensor.matmul_mx(
                out=agg_bank[(slab, g)][:],
                lhsT=route_codes[b][:, slots].bitcast(FP8X4),
                lhsT_scale=route_scales[b][:, slots],
                rhs=h_codes[u][:, cols].bitcast(FP8X4),
                rhs_scale=h_scales[u][:, cols],
                start=(c == 0),
                stop=(c == 1),
            )

        def copy_agg(slab, g, engine):
            if slab not in agg_sb:
                agg_sb[slab] = work.tile([P, 1024], F32, name="agg_sb", tag="agg_sb", bufs=4)
            copy_on(engine, agg_sb[slab][:, 512 * g : 512 * g + 512], agg_bank[(slab, g)][:])

        def store(slab, halves=(0, 1)):
            b, kt = divmod(slab, 2)
            cols = slice(512 * halves[0], 512 * halves[-1] + 512)
            nc.sync.dma_start(out=out[b, 128 * kt : 128 * kt + 128, cols], in_=agg_sb[slab][:, cols])

        regroup_list = [("copy", 0, (0,)), ("copy", 0, (1,)), ("copy", 1, (0,)), ("quantise", 0, None), ("copy", 1, (1,))]
        for u in range(2, UNITS - 1):
            regroup_list.extend([("copy", u, (0, 1)), ("quantise", u - 1, None)])
        regroup_list.extend([("copy", UNITS - 1, (0,)), ("quantise", UNITS - 2, None), ("copy", UNITS - 1, (1,))])

        def regroup_items(n):
            for i in range(n):
                if progress["regroup"] < len(regroup_list):
                    kind, u, halves = regroup_list[progress["regroup"]]
                    progress["regroup"] = progress["regroup"] + 1
                    if kind == "copy":
                        regroup_h(u, halves)
                        if halves[-1] == 1:
                            progress["regrouped"] = u
                    else:
                        quantise_h(u)
                        progress["h_quantised"] = u

        waiting = []

        def empty_slabs():
            for slab in waiting:
                for g in range(2):
                    copy_agg(slab, g, "scalar")
                store(slab)
            waiting.clear()

        def whole_slab(slab):
            for g in range(2):
                for c in range(2):
                    second_matmul(slab, g, c)
            waiting.append(slab)

        for s in range(UNITS):
            order = [(0, 0), (1, 0), (0, 1), (1, 1)]
            if s == 1:
                turn_weights()
            for jp, g in order[0:2]:
                transpose_h(s, jp, g)
                copy_ht(s, jp, g)
                if s == 0:
                    warm_up(WARM_BANK)
            if s == 0:
                regroup_items(2)
            if s == 1:
                regroup_items(1)
            if s >= 1:
                quantise_ht(s - 1)
            if s == 1:
                regroup_items(1)
                quantise_weights()
            if s >= 2:
                transpose_route(s - 2, True)
            slab = progress["multiplied"]
            if 2 * (slab // 2) + 4 <= s and progress["h_quantised"] >= 2 * (slab // 2) + 1:
                whole_slab(slab)
                progress["multiplied"] = slab + 1
            for jp, g in order[2:4]:
                transpose_h(s, jp, g)
                if s == 0:
                    warm_up(WARM_BANK)
            progress["transposed"] = s
            if s >= 2:
                copy_route(s - 2)
                regroup_items(1)
            if s >= 3 and s % 2 == 1:
                quantise_route((s - 3) // 2)
            empty_slabs()
            for jp, g in order[2:4]:
                copy_ht(s, jp, g)
            if s >= 1:
                first_matmul(s - 1, True)
            if 1 <= s < UNITS - 1:
                regroup_items(1)
            if s >= 1:
                sigmoid(s - 1)
            load_up_to(min(progress["transposed"], progress["regrouped"]) + 1 + H_BUFS)

        last = UNITS - 1
        assert progress["multiplied"] == SLABS - 4
        quantise_ht(last)
        whole_slab(SLABS - 4)
        transpose_route(last - 1, False)
        empty_slabs()
        copy_route(last - 1)
        first_matmul(last, False)
        whole_slab(SLABS - 3)
        waiting.clear()
        while progress["regroup"] < len(regroup_list) - 1:
            regroup_items(1)
        quantise_route(last // 2, (0,))
        sigmoid(last)
        transpose_route(last, False)
        copy_agg(SLABS - 3, 0, "scalar")
        copy_route(last)
        copy_agg(SLABS - 3, 1, "scalar")
        store(SLABS - 3)
        for slab in (SLABS - 2, SLABS - 1):
            for g in range(2):
                second_matmul(slab, g, 0)
        quantise_h(last, (0,))
        regroup_items(1)
        quantise_route(last // 2, (1,))
        quantise_h(last, (1,))
        for g in range(2):
            for slab in (SLABS - 2, SLABS - 1):
                second_matmul(slab, g, 1)
                copy_agg(slab, g, "vector" if slab == SLABS - 1 else "scalar")
                store(slab, (g,))
